import numpy as np
import ml_dtypes


def mxq(x, axis, fmt="e4m3"):
    dtype, down = {"e4m3": (ml_dtypes.float8_e4m3fn, 7), "e5m2": (ml_dtypes.float8_e5m2, 14)}[fmt]
    v = np.moveaxis(np.asarray(x, np.float32).astype(ml_dtypes.bfloat16).astype(np.float64), axis, -1)
    blocks = v.reshape(v.shape[:-1] + (-1, 32))
    amax = np.abs(blocks).max(-1, keepdims=True)
    byte = np.maximum(np.where(amax > 0, np.frexp(amax)[1] - 1 + 127, 0) - down, 1)
    scale = np.exp2(byte - 127.0)
    codes = (blocks / scale).astype(np.float32).astype(dtype).astype(np.float64)
    return np.moveaxis((codes * scale).reshape(v.shape), -1, axis)


WIDE = False


def mx_kscale(k):
    if not WIDE:
        return np.ones(k)
    levels = np.array([10, -10, 5, -5, 0])
    a = np.random.permutation(np.resize(levels, k // 512 * 4)).reshape(k // 512, 4)
    idx = np.arange(k)
    return np.exp2(a[idx // 512, idx % 128 // 32])


BF16 = ml_dtypes.bfloat16


def bf(x):
    return np.asarray(x, np.float32).astype(BF16)


def f64(x):
    return np.asarray(x).astype(np.float64)


B, T, D, NH, HD, QB = 8, 512, 1024, 2, 256, 512
H2 = NH // 2
HD2 = HD // 2
MXB = 32
LAMBDA_INIT = 0.8 - 0.6 * np.exp(-0.3 * 0)


def setup_inputs():
    m = np.sqrt(0.3 / HD2)
    s = f64(mx_kscale(T))
    s[:MXB] = s.max()
    q = np.random.standard_normal((B, T, NH, HD))
    k = np.random.standard_normal((B, T, NH, HD))
    q[..., 0] = np.sqrt(HD)
    k[..., 0] += np.log(s)[None, :, None]
    v = np.random.standard_normal((B, T, H2, 2 * HD)) * 2.0 * (s.max() / s)[None, :, None, None]
    return {"q_rot": bf(q),
            "k_rot": bf(k),
            "v": bf(v),
            "lambda_q1": bf(np.random.standard_normal(HD2) * 0.1 + m),
            "lambda_k1": bf(np.random.standard_normal(HD2) * 0.1 + m),
            "lambda_q2": bf(np.random.standard_normal(HD2) * 0.1 + m),
            "lambda_k2": bf(np.random.standard_normal(HD2) * 0.1 - m)}


def causal_attention(q, k, vq):
    rows = []
    for i in range(T // QB):
        lo, hi = i * QB, (i + 1) * QB
        s = q[:, :, lo:hi] @ k[:, :, :hi].transpose(0, 1, 3, 2) * (1.0 / np.sqrt(HD))
        keep = np.arange(hi)[None, :] <= np.arange(lo, hi)[:, None]
        s = np.where(keep, s, -np.inf)
        e = np.exp(s - s.max(-1, keepdims=True))
        rows.append((mxq(e, 3, "e4m3") @ vq[:, :, :hi]) / e.sum(-1, keepdims=True))
    return np.concatenate(rows, axis=2).transpose(0, 2, 1, 3)


def reference(q_rot, k_rot, v, lambda_q1, lambda_k1, lambda_q2, lambda_k2):
    q = f64(q_rot).reshape(B, T, 2, H2, HD).transpose(2, 0, 3, 1, 4)
    k = f64(k_rot).reshape(B, T, 2, H2, HD).transpose(2, 0, 3, 1, 4)
    vq = mxq(f64(v).transpose(0, 2, 1, 3), 2, "e4m3")
    y1 = causal_attention(q[0], k[0], vq)
    y2 = causal_attention(q[1], k[1], vq)
    lam1 = np.exp(np.sum(f64(lambda_q1) * f64(lambda_k1)))
    lam2 = np.exp(np.sum(f64(lambda_q2) * f64(lambda_k2)))
    lam = lam1 - lam2 + LAMBDA_INIT
    return (y1 - lam * y2).reshape(B, T, NH * HD)

@@ -1,0 +1,315 @@
+import math
+from contextlib import ExitStack
+
+import concourse.mybir as mybir
+from concourse.masks import make_identity
+
+F32 = mybir.dt.float32
+BF16 = mybir.dt.bfloat16
+U32 = mybir.dt.uint32
+U8 = mybir.dt.uint8
+FP8X4 = mybir.dt.float8_e4m3fn_x4
+ALU = mybir.AluOpType
+ACT = mybir.ActivationFunctionType
+AX = mybir.AxisListType
+
+P = 128
+PACK = 4
+B = 8
+T = 512
+GROUPS = 2
+HD = 256
+F = 512
+LAM_LEN = 128
+Q_TILES = T // P
+PAIRS = HD // 2
+SCORE_SCALE = 1.0 / math.sqrt(HD)
+LAMBDA_INIT = 0.8 - 0.6 * math.exp(-0.3 * 0)
+MASKED = -1.0e30
+
+UNITS = B * Q_TILES
+TILE_ORDER = (0, 3, 1, 2)
+AHEAD = Q_TILES
+TURN_LAG = 1
+PRODUCT_LAG = 3
+
+FLOPS = B * GROUPS * (2 * T * T * HD + 2 * T * T * F)
+
+
+def tile_mixerdiffattention_pb_t_kernel(
+    tc, q_rot, k_rot, v, lambda_q1, lambda_k1, lambda_q2, lambda_k2, out
+):
+    nc = tc.nc
+    with ExitStack() as ctx:
+        ctx.enter_context(tc.manual_schedule())
+        const = ctx.enter_context(tc.tile_pool(name="const", bufs=1))
+        loads = ctx.enter_context(tc.tile_pool(name="loads", bufs=B))
+        turned_inputs = ctx.enter_context(tc.tile_pool(name="turned_inputs", bufs=2 * GROUPS))
+        values = ctx.enter_context(tc.tile_pool(name="values", bufs=3))
+        grouped = ctx.enter_context(tc.tile_pool(name="grouped", bufs=3))
+        quantised = ctx.enter_context(tc.tile_pool(name="quantised", bufs=PRODUCT_LAG + 2))
+        stats = ctx.enter_context(tc.tile_pool(name="stats", bufs=PRODUCT_LAG + 3))
+        results = ctx.enter_context(tc.tile_pool(name="results", bufs=4))
+        turned_psum = ctx.enter_context(tc.psum_pool(name="turned_psum", bufs=2))
+        score_psum = ctx.enter_context(tc.psum_pool(name="score_psum", bufs=4))
+        y_psum = ctx.enter_context(tc.psum_pool(name="y_psum", bufs=2))
+
+        ident_f32 = const.tile([P, P], F32)
+        make_identity(nc, ident_f32[:])
+        ident_bf16 = const.tile([P, P], BF16)
+        make_identity(nc, ident_bf16[:])
+        mask_f32 = const.tile([P, P], F32)
+        nc.gpsimd.memset(mask_f32[:], 0.0)
+        nc.gpsimd.affine_select(
+            out=mask_f32[:],
+            in_=mask_f32[:],
+            compare_op=ALU.is_ge,
+            fill=MASKED,
+            base=0,
+            pattern=[[-1, P]],
+            channel_multiplier=1,
+        )
+        mask_bf16 = const.tile([P, P], BF16)
+        nc.vector.tensor_copy(out=mask_bf16[:], in_=mask_f32[:])
+        zero_column = const.tile([P, 1], F32)
+        nc.vector.memset(zero_column[:], 0.0)
+        one_column = const.tile([P, 1], F32)
+        nc.scalar.activation(out=one_column[:], in_=zero_column[:], func=ACT.Exp)
+
+        e_fixed = []
+        for i in range(Q_TILES):
+            e_tile = const.tile([P, GROUPS, 2, T // 2], BF16, name="e_tile%d" % i)
+            nc.vector.memset(e_tile[:], 0.0)
+            e_fixed.append(e_tile)
+
+        q_in, k_in, v_in = [], [], []
+        lam_in = const.tile([P, 4, LAM_LEN], BF16)
+        for b in range(B):
+            k_sb = loads.tile([P, Q_TILES, GROUPS * HD], BF16, tag="k")
+            nc.sync.dma_start(out=k_sb[:], in_=k_rot[b].rearrange("(j p) h d -> p j (h d)", p=P))
+            q_sb = loads.tile([P, Q_TILES, GROUPS * HD], BF16, tag="q")
+            nc.sync.dma_start(out=q_sb[:], in_=q_rot[b].rearrange("(j p) h d -> p j (h d)", p=P))
+            if b == 0:
+                for n, vec in enumerate((lambda_q1, lambda_q2, lambda_k1, lambda_k2)):
+                    nc.sync.dma_start(out=lam_in[:, n, :], in_=vec.partition_broadcast(P))
+            v_sb = loads.tile([P, PACK, F], BF16, tag="v")
+            nc.sync.dma_start(out=v_sb[:], in_=v[b].rearrange("(p t) o f -> p t (o f)", t=PACK))
+            q_in.append(q_sb)
+            k_in.append(k_sb)
+            v_in.append(v_sb)
+            for g in (1, 0):
+                q_head = q_sb[:, :, g * HD : (g + 1) * HD]
+                nc.gpsimd.tensor_scalar(
+                    out=q_head,
+                    in0=q_head,
+                    scalar1=SCORE_SCALE,
+                    scalar2=0.0,
+                    op0=ALU.mult,
+                    op1=ALU.add,
+                )
+
+        neg_lam = const.tile([P, 1], F32)
+
+        def compute_neg_lam():
+            products = const.tile([P, 2, LAM_LEN], F32)
+            nc.vector.tensor_tensor(
+                out=products[:], in0=lam_in[:, 0:2, :], in1=lam_in[:, 2:4, :], op=ALU.mult
+            )
+            dots = const.tile([P, 2], F32)
+            nc.vector.reduce_sum(out=dots[:], in_=products[:], axis=AX.X)
+            exp_dots = const.tile([P, 2], F32)
+            nc.scalar.activation(out=exp_dots[:], in_=dots[:], func=ACT.Exp)
+            nc.vector.tensor_scalar(
+                out=neg_lam[:],
+                in0=exp_dots[:, 1:2],
+                scalar1=exp_dots[:, 0:1],
+                scalar2=-LAMBDA_INIT,
+                op0=ALU.subtract,
+                op1=ALU.add,
+            )
+
+        qT, kT = {}, {}
+        v_grouped, v_codes, v_scales = {}, {}, {}
+        s_banks, neg_max, row_sum, weight = {}, {}, {}, {}
+        eT_banks, e_grouped, e_codes, e_scales = {}, {}, {}, {}
+        y_banks, out_tiles = {}, {}
+
+        def live(u):
+            return 0 <= u < UNITS
+
+        def turn_input(u):
+            b, quarter = divmod(u, Q_TILES)
+            g = 1 - quarter // 2
+            source, turned = ((k_in, kT), (q_in, qT))[quarter % 2]
+            words = source[b][:].bitcast(F32)
+            bank = turned_psum.tile([P, T], F32, tag="turned")
+            for j in range(Q_TILES):
+                nc.tensor.transpose(
+                    bank[:, j * P : (j + 1) * P], words[:, j, g * PAIRS : (g + 1) * PAIRS], ident_f32[:]
+                )
+            rows = turned_inputs.tile([P, T, 2], BF16, tag="turned%d" % (quarter % 2))
+            nc.scalar.copy(out=rows[:].rearrange("p r c -> p (r c)"), in_=bank[:].bitcast(BF16))
+            turned[b, g] = rows
+
+        def regroup_values(u):
+            b, quarter = divmod(u, Q_TILES)
+            side_by_side = values.tile([P, P, PACK], BF16, align_bytes=64)
+            nc.vector.tensor_copy(
+                out=side_by_side[:].rearrange("p (n i) t -> p n t i", i=4),
+                in_=v_in[b][:, :, quarter * P : (quarter + 1) * P].rearrange(
+                    "p t (n i) -> p n t i", i=4
+                ),
+            )
+            v_grouped[u] = side_by_side
+
+        def quantise_values(u):
+            b, quarter = divmod(u, Q_TILES)
+            if quarter == 0:
+                codes = values.tile([P, F], U32, align_bytes=64)
+                scales = values.tile([P, F], U8, align_bytes=64)
+                v_codes[b], v_scales[b] = codes, scales
+            features = slice(quarter * P, (quarter + 1) * P)
+            nc.vector.quantize_mx(
+                out=v_codes[b][:, features].bitcast(FP8X4),
+                scales=v_scales[b][:, features],
+                in_=v_grouped[u][:].rearrange("p f t -> p (f t)"),
+            )
+
+        def scores(h):
+            u, n = divmod(h, GROUPS)
+            b, i, g = u // Q_TILES, TILE_ORDER[u % Q_TILES], 1 - n
+            rows = slice(i * P, (i + 1) * P)
+            n_keys = (i + 1) * P
+            bank = score_psum.tile([P, T], F32, tag="scores")
+            nc.tensor.matmul(
+                bank[:, :n_keys], lhsT=qT[b, g][:, rows, 0], rhs=kT[b, g][:, :n_keys, 0], start=True, stop=False
+            )
+            nc.tensor.matmul(bank[:, rows], lhsT=ident_bf16[:], rhs=mask_bf16[:], start=False, stop=False)
+            nc.tensor.matmul(
+                bank[:, :n_keys], lhsT=qT[b, g][:, rows, 1], rhs=kT[b, g][:, :n_keys, 1], start=False, stop=True
+            )
+            s_banks[h] = bank
+
+        def row_maximum(h):
+            u, n = divmod(h, GROUPS)
+            n_keys = (TILE_ORDER[u % Q_TILES] + 1) * P
+            if n == 0:
+                maxima = stats.tile([P, GROUPS], F32)
+                neg_max[u] = maxima
+            nc.vector.reduce_max(
+                out=neg_max[u][:, n : n + 1], in_=s_banks[h][:, :n_keys], axis=AX.X, negate=True
+            )
+
+        def numerators(h):
+            u, n = divmod(h, GROUPS)
+            i = TILE_ORDER[u % Q_TILES]
+            n_keys = (i + 1) * P
+            if n == 0:
+                sums = stats.tile([P, GROUPS], F32)
+                row_sum[u] = sums
+            nc.scalar.activation(
+                out=e_fixed[i][:, n, :, : n_keys // 2].rearrange("p u (w c) -> p u w c", c=2),
+                in_=s_banks[h][:, :n_keys].rearrange("p (w u c) -> p u w c", u=2, c=2),
+                func=ACT.Exp,
+                bias=neg_max[u][:, n : n + 1],
+                accum_out=row_sum[u][:, n : n + 1],
+            )
+
+        def weights(u):
+            factors = stats.tile([P, GROUPS], F32)
+            nc.vector.reciprocal(out=factors[:], in_=row_sum[u][:])
+            nc.vector.tensor_scalar_mul(out=factors[:, 0:1], in0=factors[:, 0:1], scalar1=neg_lam[:, 0:1])
+            weight[u] = factors
+
+        def turn_e(u):
+            e_words = e_fixed[TILE_ORDER[u % Q_TILES]][:].bitcast(F32)
+            bank = turned_psum.tile([P, T], F32, tag="turned")
+            for n in range(GROUPS):
+                for plane in range(2):
+                    nc.tensor.transpose(
+                        bank[:, (2 * n + plane) * P : (2 * n + plane + 1) * P],
+                        e_words[:, n, plane, :],
+                        ident_f32[:],
+                    )
+            side_by_side = grouped.tile([P, GROUPS * P, PACK], BF16, align_bytes=64)
+            copy = nc.vector.tensor_copy if u % 2 == 0 else nc.scalar.copy
+            copy(
+                out=side_by_side[:].bitcast(F32).rearrange("p (n r) u -> p n r u", n=GROUPS),
+                in_=bank[:].rearrange("p (n u r) -> p n r u", n=GROUPS, u=2),
+            )
+            e_grouped[u] = side_by_side
+
+        def quantise_e(u):
+            codes = quantised.tile([P, GROUPS * P], U32, align_bytes=64)
+            scales = quantised.tile([P, GROUPS * P], U8, align_bytes=64)
+            nc.vector.quantize_mx(
+                out=codes[:].bitcast(FP8X4),
+                scales=scales[:],
+                in_=e_grouped[u][:].rearrange("p r t -> p (r t)"),
+            )
+            e_codes[u], e_scales[u] = codes, scales
+
+        def products(u):
+            b = u // Q_TILES
+            for n in range(GROUPS):
+                bank = y_psum.tile([P, F], F32, tag="y")
+                nc.tensor.matmul_mx(
+                    out=bank[:],
+                    lhsT=e_codes[u][:, n * P : (n + 1) * P].bitcast(FP8X4),
+                    lhsT_scale=e_scales[u][:, n * P : (n + 1) * P],
+                    rhs=v_codes[b][:].bitcast(FP8X4),
+                    rhs_scale=v_scales[b][:],
+                    start=True,
+                    stop=True,
+                )
+                y_banks[u, n] = bank
+
+        def weigh_group_2(u):
+            result = results.tile([P, F], F32)
+            nc.scalar.activation(out=result[:], in_=y_banks[u, 0][:], func=ACT.Copy, scale=weight[u][:, 0:1])
+            out_tiles[u] = result
+
+        def add_group_1_and_store(u):
+            b, i = u // Q_TILES, TILE_ORDER[u % Q_TILES]
+            nc.vector.scalar_tensor_tensor(
+                out=out_tiles[u][:],
+                in0=y_banks[u, 1][:],
+                scalar=weight[u][:, 1:2],
+                in1=out_tiles[u][:],
+                op0=ALU.mult,
+                op1=ALU.add,
+            )
+            nc.sync.dma_start(out=out[b, i * P : (i + 1) * P, :], in_=out_tiles[u][:])
+
+        def step(t):
+            if live(t + AHEAD):
+                regroup_values(t + AHEAD)
+            if live(t - PRODUCT_LAG):
+                products(t - PRODUCT_LAG)
+                weigh_group_2(t - PRODUCT_LAG)
+            if live(t):
+                scores(2 * t + 1)
+                row_maximum(2 * t + 1)
+                numerators(2 * t)
+            if live(t - PRODUCT_LAG):
+                add_group_1_and_store(t - PRODUCT_LAG)
+            if live(t + AHEAD):
+                turn_input(t + AHEAD)
+            if live(t - TURN_LAG):
+                turn_e(t - TURN_LAG)
+            if live(t + 1):
+                scores(2 * t + 2)
+                row_maximum(2 * t + 2)
+            if live(t):
+                numerators(2 * t + 1)
+            if live(t - TURN_LAG):
+                quantise_e(t - TURN_LAG)
+                weights(t - TURN_LAG)
+            if live(t + AHEAD):
+                quantise_values(t + AHEAD)
+
+        for t in range(-AHEAD, 0):
+            step(t)
+        compute_neg_lam()
+        for t in range(0, UNITS + PRODUCT_LAG):
+            step(t)

@@ -85,10 +85,23 @@ def tile_mixerdiffattention_pb_t_kernel(
         q_in, k_in, v_in = [], [], []
         lam_in = const.tile([P, 4, LAM_LEN], BF16)
         for b in range(B):
-            k_sb = loads.tile([P, Q_TILES, GROUPS * HD], BF16, tag="k")
-            nc.sync.dma_start(out=k_sb[:], in_=k_rot[b].rearrange("(j p) h d -> p j (h d)", p=P))
-            q_sb = loads.tile([P, Q_TILES, GROUPS * HD], BF16, tag="q")
-            nc.sync.dma_start(out=q_sb[:], in_=q_rot[b].rearrange("(j p) h d -> p j (h d)", p=P))
+            q_sb = loads.tile([P, Q_TILES, GROUPS, HD], BF16, tag="q")
+            k_sb = loads.tile([P, Q_TILES, GROUPS, HD], BF16, tag="k")
+            for g in (1, 0):
+                nc.sync.dma_start(
+                    out=q_sb[:, :, g, :], in_=q_rot[b, :, g, :].rearrange("(j p) d -> p j d", p=P)
+                )
+                nc.sync.dma_start(
+                    out=k_sb[:, :, g, :], in_=k_rot[b, :, g, :].rearrange("(j p) d -> p j d", p=P)
+                )
+                nc.gpsimd.tensor_scalar(
+                    out=q_sb[:, :, g, :],
+                    in0=q_sb[:, :, g, :],
+                    scalar1=SCORE_SCALE,
+                    scalar2=0.0,
+                    op0=ALU.mult,
+                    op1=ALU.add,
+                )
             if b == 0:
                 for n, vec in enumerate((lambda_q1, lambda_q2, lambda_k1, lambda_k2)):
                     nc.sync.dma_start(out=lam_in[:, n, :], in_=vec.partition_broadcast(P))
@@ -97,16 +110,6 @@ def tile_mixerdiffattention_pb_t_kernel(
             q_in.append(q_sb)
             k_in.append(k_sb)
             v_in.append(v_sb)
-            for g in (1, 0):
-                q_head = q_sb[:, :, g * HD : (g + 1) * HD]
-                nc.gpsimd.tensor_scalar(
-                    out=q_head,
-                    in0=q_head,
-                    scalar1=SCORE_SCALE,
-                    scalar2=0.0,
-                    op0=ALU.mult,
-                    op1=ALU.add,
-                )
 
         neg_lam = const.tile([P, 1], F32)
 
@@ -144,11 +147,9 @@ def tile_mixerdiffattention_pb_t_kernel(
             words = source[b][:].bitcast(F32)
             bank = turned_psum.tile([P, T], F32, tag="turned")
             for j in range(Q_TILES):
-                nc.tensor.transpose(
-                    bank[:, j * P : (j + 1) * P], words[:, j, g * PAIRS : (g + 1) * PAIRS], ident_f32[:]
-                )
+                nc.tensor.transpose(bank[:, j * P : (j + 1) * P], words[:, j, g, :], ident_f32[:])
             rows = turned_inputs.tile([P, T, 2], BF16, tag="turned%d" % (quarter % 2))
-            nc.scalar.copy(out=rows[:].rearrange("p r c -> p (r c)"), in_=bank[:].bitcast(BF16))
+            nc.scalar.copy(out=rows[:].bitcast(F32).rearrange("p r w -> p (r w)"), in_=bank[:])
             turned[b, g] = rows
 
         def regroup_values(u):
@@ -218,8 +219,12 @@ def tile_mixerdiffattention_pb_t_kernel(
         def weights(u):
             factors = stats.tile([P, GROUPS], F32)
             nc.vector.reciprocal(out=factors[:], in_=row_sum[u][:])
-            nc.vector.tensor_scalar_mul(out=factors[:, 0:1], in0=factors[:, 0:1], scalar1=neg_lam[:, 0:1])
             weight[u] = factors
+
+        def weight_group_2(u):
+            nc.vector.tensor_scalar_mul(
+                out=weight[u][:, 0:1], in0=weight[u][:, 0:1], scalar1=neg_lam[:, 0:1]
+            )
 
         def turn_e(u):
             e_words = e_fixed[TILE_ORDER[u % Q_TILES]][:].bitcast(F32)
@@ -307,6 +312,8 @@ def tile_mixerdiffattention_pb_t_kernel(
                 weights(t - TURN_LAG)
             if live(t + AHEAD):
                 quantise_values(t + AHEAD)
+            if live(t - TURN_LAG):
+                weight_group_2(t - TURN_LAG)
 
         for t in range(-AHEAD, 0):
             step(t)

@@ -29,9 +29,12 @@ MASKED = -1.0e30
 
 UNITS = B * Q_TILES
 TILE_ORDER = (0, 3, 1, 2)
-AHEAD = Q_TILES
+INPUTS_AHEAD = 5
+VALUES_AHEAD = 2
 TURN_LAG = 1
-PRODUCT_LAG = 3
+QUANTISE_LAG = 2
+GROUP_2_LAG = 4
+GROUP_1_LAG = 5
 
 FLOPS = B * GROUPS * (2 * T * T * HD + 2 * T * T * F)
 
@@ -46,13 +49,14 @@ def tile_mixerdiffattention_pb_t_kernel(
         loads = ctx.enter_context(tc.tile_pool(name="loads", bufs=B))
         turned_inputs = ctx.enter_context(tc.tile_pool(name="turned_inputs", bufs=2 * GROUPS))
         values = ctx.enter_context(tc.tile_pool(name="values", bufs=3))
+        regrouped = ctx.enter_context(tc.tile_pool(name="regrouped", bufs=1))
         grouped = ctx.enter_context(tc.tile_pool(name="grouped", bufs=3))
-        quantised = ctx.enter_context(tc.tile_pool(name="quantised", bufs=PRODUCT_LAG + 2))
-        stats = ctx.enter_context(tc.tile_pool(name="stats", bufs=PRODUCT_LAG + 3))
+        quantised = ctx.enter_context(tc.tile_pool(name="quantised", bufs=GROUP_1_LAG))
+        stats = ctx.enter_context(tc.tile_pool(name="stats", bufs=GROUP_1_LAG + 2))
         results = ctx.enter_context(tc.tile_pool(name="results", bufs=4))
         turned_psum = ctx.enter_context(tc.psum_pool(name="turned_psum", bufs=2))
-        score_psum = ctx.enter_context(tc.psum_pool(name="score_psum", bufs=4))
-        y_psum = ctx.enter_context(tc.psum_pool(name="y_psum", bufs=2))
+        score_psum = ctx.enter_context(tc.psum_pool(name="score_psum", bufs=3))
+        y_psum = ctx.enter_context(tc.psum_pool(name="y_psum", bufs=3))
 
         ident_f32 = const.tile([P, P], F32)
         make_identity(nc, ident_f32[:])
@@ -85,23 +89,10 @@ def tile_mixerdiffattention_pb_t_kernel(
         q_in, k_in, v_in = [], [], []
         lam_in = const.tile([P, 4, LAM_LEN], BF16)
         for b in range(B):
-            q_sb = loads.tile([P, Q_TILES, GROUPS, HD], BF16, tag="q")
-            k_sb = loads.tile([P, Q_TILES, GROUPS, HD], BF16, tag="k")
-            for g in (1, 0):
-                nc.sync.dma_start(
-                    out=q_sb[:, :, g, :], in_=q_rot[b, :, g, :].rearrange("(j p) d -> p j d", p=P)
-                )
-                nc.sync.dma_start(
-                    out=k_sb[:, :, g, :], in_=k_rot[b, :, g, :].rearrange("(j p) d -> p j d", p=P)
-                )
-                nc.gpsimd.tensor_scalar(
-                    out=q_sb[:, :, g, :],
-                    in0=q_sb[:, :, g, :],
-                    scalar1=SCORE_SCALE,
-                    scalar2=0.0,
-                    op0=ALU.mult,
-                    op1=ALU.add,
-                )
+            q_sb = loads.tile([P, Q_TILES, GROUPS * HD], BF16, tag="q")
+            nc.sync.dma_start(out=q_sb[:], in_=q_rot[b].rearrange("(j p) h d -> p j (h d)", p=P))
+            k_sb = loads.tile([P, Q_TILES, GROUPS * HD], BF16, tag="k")
+            nc.sync.dma_start(out=k_sb[:], in_=k_rot[b].rearrange("(j p) h d -> p j (h d)", p=P))
             if b == 0:
                 for n, vec in enumerate((lambda_q1, lambda_q2, lambda_k1, lambda_k2)):
                     nc.sync.dma_start(out=lam_in[:, n, :], in_=vec.partition_broadcast(P))
@@ -140,6 +131,9 @@ def tile_mixerdiffattention_pb_t_kernel(
         def live(u):
             return 0 <= u < UNITS
 
+        def scale_queries(b):
+            nc.vector.tensor_scalar_mul(out=q_in[b][:], in0=q_in[b][:], scalar1=SCORE_SCALE)
+
         def turn_input(u):
             b, quarter = divmod(u, Q_TILES)
             g = 1 - quarter // 2
@@ -147,21 +141,25 @@ def tile_mixerdiffattention_pb_t_kernel(
             words = source[b][:].bitcast(F32)
             bank = turned_psum.tile([P, T], F32, tag="turned")
             for j in range(Q_TILES):
-                nc.tensor.transpose(bank[:, j * P : (j + 1) * P], words[:, j, g, :], ident_f32[:])
+                nc.tensor.transpose(
+                    bank[:, j * P : (j + 1) * P], words[:, j, g * PAIRS : (g + 1) * PAIRS], ident_f32[:]
+                )
             rows = turned_inputs.tile([P, T, 2], BF16, tag="turned%d" % (quarter % 2))
             nc.scalar.copy(out=rows[:].bitcast(F32).rearrange("p r w -> p (r w)"), in_=bank[:])
             turned[b, g] = rows
 
         def regroup_values(u):
             b, quarter = divmod(u, Q_TILES)
-            side_by_side = values.tile([P, P, PACK], BF16, align_bytes=64)
-            nc.vector.tensor_copy(
-                out=side_by_side[:].rearrange("p (n i) t -> p n t i", i=4),
-                in_=v_in[b][:, :, quarter * P : (quarter + 1) * P].rearrange(
-                    "p t (n i) -> p n t i", i=4
-                ),
+            keys_together = regrouped.tile([P, P, PACK], BF16, align_bytes=64)
+            nc.gpsimd.tensor_scalar(
+                out=keys_together[:],
+                in0=v_in[b][:, :, quarter * P : (quarter + 1) * P].rearrange("p t f -> p f t"),
+                scalar1=1.0,
+                scalar2=0.0,
+                op0=ALU.mult,
+                op1=ALU.add,
             )
-            v_grouped[u] = side_by_side
+            v_grouped[u] = keys_together
 
         def quantise_values(u):
             b, quarter = divmod(u, Q_TILES)
@@ -254,20 +252,19 @@ def tile_mixerdiffattention_pb_t_kernel(
             )
             e_codes[u], e_scales[u] = codes, scales
 
-        def products(u):
+        def product(u, n):
             b = u // Q_TILES
-            for n in range(GROUPS):
-                bank = y_psum.tile([P, F], F32, tag="y")
-                nc.tensor.matmul_mx(
-                    out=bank[:],
-                    lhsT=e_codes[u][:, n * P : (n + 1) * P].bitcast(FP8X4),
-                    lhsT_scale=e_scales[u][:, n * P : (n + 1) * P],
-                    rhs=v_codes[b][:].bitcast(FP8X4),
-                    rhs_scale=v_scales[b][:],
-                    start=True,
-                    stop=True,
-                )
-                y_banks[u, n] = bank
+            bank = y_psum.tile([P, F], F32, tag="y")
+            nc.tensor.matmul_mx(
+                out=bank[:],
+                lhsT=e_codes[u][:, n * P : (n + 1) * P].bitcast(FP8X4),
+                lhsT_scale=e_scales[u][:, n * P : (n + 1) * P],
+                rhs=v_codes[b][:].bitcast(FP8X4),
+                rhs_scale=v_scales[b][:],
+                start=True,
+                stop=True,
+            )
+            y_banks[u, n] = bank
 
         def weigh_group_2(u):
             result = results.tile([P, F], F32)
@@ -287,19 +284,24 @@ def tile_mixerdiffattention_pb_t_kernel(
             nc.sync.dma_start(out=out[b, i * P : (i + 1) * P, :], in_=out_tiles[u][:])
 
         def step(t):
-            if live(t + AHEAD):
-                regroup_values(t + AHEAD)
-            if live(t - PRODUCT_LAG):
-                products(t - PRODUCT_LAG)
-                weigh_group_2(t - PRODUCT_LAG)
+            if live(t + INPUTS_AHEAD) and (t + INPUTS_AHEAD) % Q_TILES == 0:
+                scale_queries((t + INPUTS_AHEAD) // Q_TILES)
+            if live(t + VALUES_AHEAD):
+                regroup_values(t + VALUES_AHEAD)
+            if live(t - GROUP_2_LAG):
+                product(t - GROUP_2_LAG, 0)
+            if live(t - GROUP_1_LAG):
+                product(t - GROUP_1_LAG, 1)
+            if live(t - GROUP_2_LAG):
+                weigh_group_2(t - GROUP_2_LAG)
             if live(t):
                 scores(2 * t + 1)
                 row_maximum(2 * t + 1)
                 numerators(2 * t)
-            if live(t - PRODUCT_LAG):
-                add_group_1_and_store(t - PRODUCT_LAG)
-            if live(t + AHEAD):
-                turn_input(t + AHEAD)
+            if live(t - GROUP_1_LAG):
+                add_group_1_and_store(t - GROUP_1_LAG)
+            if live(t + INPUTS_AHEAD):
+                turn_input(t + INPUTS_AHEAD)
             if live(t - TURN_LAG):
                 turn_e(t - TURN_LAG)
             if live(t + 1):
@@ -307,16 +309,17 @@ def tile_mixerdiffattention_pb_t_kernel(
                 row_maximum(2 * t + 2)
             if live(t):
                 numerators(2 * t + 1)
+            if live(t - QUANTISE_LAG):
+                quantise_e(t - QUANTISE_LAG)
             if live(t - TURN_LAG):
-                quantise_e(t - TURN_LAG)
                 weights(t - TURN_LAG)
-            if live(t + AHEAD):
-                quantise_values(t + AHEAD)
+            if live(t + VALUES_AHEAD):
+                quantise_values(t + VALUES_AHEAD)
             if live(t - TURN_LAG):
                 weight_group_2(t - TURN_LAG)
 
-        for t in range(-AHEAD, 0):
+        for t in range(-INPUTS_AHEAD, 0):
             step(t)
         compute_neg_lam()
-        for t in range(0, UNITS + PRODUCT_LAG):
+        for t in range(0, UNITS + GROUP_1_LAG):
             step(t)

@@ -23,13 +23,16 @@ F = 512
 LAM_LEN = 128
 Q_TILES = T // P
 PAIRS = HD // 2
+PLANES = 2
 SCORE_SCALE = 1.0 / math.sqrt(HD)
 LAMBDA_INIT = 0.8 - 0.6 * math.exp(-0.3 * 0)
 MASKED = -1.0e30
 
 UNITS = B * Q_TILES
+HEAD_AT_PLACE = (1, 0)
 TILE_ORDER = (0, 3, 1, 2)
-INPUTS_AHEAD = 5
+
+INPUTS_AHEAD = Q_TILES
 VALUES_AHEAD = 2
 TURN_LAG = 1
 QUANTISE_LAG = 2
@@ -45,13 +48,14 @@ def tile_mixerdiffattention_pb_t_kernel(
     nc = tc.nc
     with ExitStack() as ctx:
         ctx.enter_context(tc.manual_schedule())
+
         const = ctx.enter_context(tc.tile_pool(name="const", bufs=1))
         loads = ctx.enter_context(tc.tile_pool(name="loads", bufs=B))
         turned_inputs = ctx.enter_context(tc.tile_pool(name="turned_inputs", bufs=2 * GROUPS))
-        values = ctx.enter_context(tc.tile_pool(name="values", bufs=3))
         regrouped = ctx.enter_context(tc.tile_pool(name="regrouped", bufs=1))
-        grouped = ctx.enter_context(tc.tile_pool(name="grouped", bufs=3))
-        quantised = ctx.enter_context(tc.tile_pool(name="quantised", bufs=GROUP_1_LAG))
+        values = ctx.enter_context(tc.tile_pool(name="values", bufs=3))
+        grouped = ctx.enter_context(tc.tile_pool(name="grouped", bufs=QUANTISE_LAG - TURN_LAG + 2))
+        quantised = ctx.enter_context(tc.tile_pool(name="quantised", bufs=GROUP_1_LAG - QUANTISE_LAG + 2))
         stats = ctx.enter_context(tc.tile_pool(name="stats", bufs=GROUP_1_LAG + 2))
         results = ctx.enter_context(tc.tile_pool(name="results", bufs=4))
         turned_psum = ctx.enter_context(tc.psum_pool(name="turned_psum", bufs=2))
@@ -82,7 +86,7 @@ def tile_mixerdiffattention_pb_t_kernel(
 
         e_fixed = []
         for i in range(Q_TILES):
-            e_tile = const.tile([P, GROUPS, 2, T // 2], BF16, name="e_tile%d" % i)
+            e_tile = const.tile([P, GROUPS, PLANES, T // PLANES], BF16, name="e_tile%d" % i)
             nc.vector.memset(e_tile[:], 0.0)
             e_fixed.append(e_tile)
 
@@ -125,7 +129,7 @@ def tile_mixerdiffattention_pb_t_kernel(
         qT, kT = {}, {}
         v_grouped, v_codes, v_scales = {}, {}, {}
         s_banks, neg_max, row_sum, weight = {}, {}, {}, {}
-        eT_banks, e_grouped, e_codes, e_scales = {}, {}, {}, {}
+        e_grouped, e_codes, e_scales = {}, {}, {}
         y_banks, out_tiles = {}, {}
 
         def live(u):
@@ -136,17 +140,20 @@ def tile_mixerdiffattention_pb_t_kernel(
 
         def turn_input(u):
             b, quarter = divmod(u, Q_TILES)
-            g = 1 - quarter // 2
+            place = quarter // 2
             source, turned = ((k_in, kT), (q_in, qT))[quarter % 2]
             words = source[b][:].bitcast(F32)
+            head = HEAD_AT_PLACE[place]
             bank = turned_psum.tile([P, T], F32, tag="turned")
             for j in range(Q_TILES):
                 nc.tensor.transpose(
-                    bank[:, j * P : (j + 1) * P], words[:, j, g * PAIRS : (g + 1) * PAIRS], ident_f32[:]
+                    bank[:, j * P : (j + 1) * P],
+                    words[:, j, head * PAIRS : (head + 1) * PAIRS],
+                    ident_f32[:],
                 )
             rows = turned_inputs.tile([P, T, 2], BF16, tag="turned%d" % (quarter % 2))
             nc.scalar.copy(out=rows[:].bitcast(F32).rearrange("p r w -> p (r w)"), in_=bank[:])
-            turned[b, g] = rows
+            turned[b, place] = rows
 
         def regroup_values(u):
             b, quarter = divmod(u, Q_TILES)
@@ -175,46 +182,47 @@ def tile_mixerdiffattention_pb_t_kernel(
             )
 
         def scores(h):
-            u, n = divmod(h, GROUPS)
-            b, i, g = u // Q_TILES, TILE_ORDER[u % Q_TILES], 1 - n
+            u, place = divmod(h, GROUPS)
+            b, i = u // Q_TILES, TILE_ORDER[u % Q_TILES]
             rows = slice(i * P, (i + 1) * P)
             n_keys = (i + 1) * P
+            queries, keys = qT[b, place], kT[b, place]
             bank = score_psum.tile([P, T], F32, tag="scores")
             nc.tensor.matmul(
-                bank[:, :n_keys], lhsT=qT[b, g][:, rows, 0], rhs=kT[b, g][:, :n_keys, 0], start=True, stop=False
+                bank[:, :n_keys], lhsT=queries[:, rows, 0], rhs=keys[:, :n_keys, 0], start=True, stop=False
             )
             nc.tensor.matmul(bank[:, rows], lhsT=ident_bf16[:], rhs=mask_bf16[:], start=False, stop=False)
             nc.tensor.matmul(
-                bank[:, :n_keys], lhsT=qT[b, g][:, rows, 1], rhs=kT[b, g][:, :n_keys, 1], start=False, stop=True
+                bank[:, :n_keys], lhsT=queries[:, rows, 1], rhs=keys[:, :n_keys, 1], start=False, stop=True
             )
             s_banks[h] = bank
 
         def row_maximum(h):
-            u, n = divmod(h, GROUPS)
+            u, place = divmod(h, GROUPS)
             n_keys = (TILE_ORDER[u % Q_TILES] + 1) * P
-            if n == 0:
+            if place == 0:
                 maxima = stats.tile([P, GROUPS], F32)
                 neg_max[u] = maxima
             nc.vector.reduce_max(
-                out=neg_max[u][:, n : n + 1], in_=s_banks[h][:, :n_keys], axis=AX.X, negate=True
+                out=neg_max[u][:, place : place + 1], in_=s_banks[h][:, :n_keys], axis=AX.X, negate=True
             )
 
         def numerators(h):
-            u, n = divmod(h, GROUPS)
+            u, place = divmod(h, GROUPS)
             i = TILE_ORDER[u % Q_TILES]
             n_keys = (i + 1) * P
-            if n == 0:
+            if place == 0:
                 sums = stats.tile([P, GROUPS], F32)
                 row_sum[u] = sums
             nc.scalar.activation(
-                out=e_fixed[i][:, n, :, : n_keys // 2].rearrange("p u (w c) -> p u w c", c=2),
-                in_=s_banks[h][:, :n_keys].rearrange("p (w u c) -> p u w c", u=2, c=2),
+                out=e_fixed[i][:, place, :, : n_keys // PLANES].rearrange("p a (w c) -> p a w c", c=2),
+                in_=s_banks[h][:, :n_keys].rearrange("p (w a c) -> p a w c", a=PLANES, c=2),
                 func=ACT.Exp,
-                bias=neg_max[u][:, n : n + 1],
-                accum_out=row_sum[u][:, n : n + 1],
+                bias=neg_max[u][:, place : place + 1],
+                accum_out=row_sum[u][:, place : place + 1],
             )
 
-        def weights(u):
+        def invert_row_sums(u):
             factors = stats.tile([P, GROUPS], F32)
             nc.vector.reciprocal(out=factors[:], in_=row_sum[u][:])
             weight[u] = factors
@@ -227,20 +235,19 @@ def tile_mixerdiffattention_pb_t_kernel(
         def turn_e(u):
             e_words = e_fixed[TILE_ORDER[u % Q_TILES]][:].bitcast(F32)
             bank = turned_psum.tile([P, T], F32, tag="turned")
-            for n in range(GROUPS):
-                for plane in range(2):
+            for place in range(GROUPS):
+                for plane in range(PLANES):
+                    column = (PLANES * place + plane) * P
                     nc.tensor.transpose(
-                        bank[:, (2 * n + plane) * P : (2 * n + plane + 1) * P],
-                        e_words[:, n, plane, :],
-                        ident_f32[:],
+                        bank[:, column : column + P], e_words[:, place, plane, :], ident_f32[:]
                     )
-            side_by_side = grouped.tile([P, GROUPS * P, PACK], BF16, align_bytes=64)
+            keys_together = grouped.tile([P, GROUPS * P, PACK], BF16, align_bytes=64)
             copy = nc.vector.tensor_copy if u % 2 == 0 else nc.scalar.copy
             copy(
-                out=side_by_side[:].bitcast(F32).rearrange("p (n r) u -> p n r u", n=GROUPS),
-                in_=bank[:].rearrange("p (n u r) -> p n r u", n=GROUPS, u=2),
+                out=keys_together[:].bitcast(F32).rearrange("p (n r) a -> p n r a", n=GROUPS),
+                in_=bank[:].rearrange("p (n a r) -> p n r a", n=GROUPS, a=PLANES),
             )
-            e_grouped[u] = side_by_side
+            e_grouped[u] = keys_together
 
         def quantise_e(u):
             codes = quantised.tile([P, GROUPS * P], U32, align_bytes=64)
@@ -252,30 +259,33 @@ def tile_mixerdiffattention_pb_t_kernel(
             )
             e_codes[u], e_scales[u] = codes, scales
 
-        def product(u, n):
+        def product(u, place):
             b = u // Q_TILES
+            queries = slice(place * P, (place + 1) * P)
             bank = y_psum.tile([P, F], F32, tag="y")
             nc.tensor.matmul_mx(
                 out=bank[:],
-                lhsT=e_codes[u][:, n * P : (n + 1) * P].bitcast(FP8X4),
-                lhsT_scale=e_scales[u][:, n * P : (n + 1) * P],
+                lhsT=e_codes[u][:, queries].bitcast(FP8X4),
+                lhsT_scale=e_scales[u][:, queries],
                 rhs=v_codes[b][:].bitcast(FP8X4),
                 rhs_scale=v_scales[b][:],
                 start=True,
                 stop=True,
             )
-            y_banks[u, n] = bank
+            y_banks[GROUPS * u + place] = bank
 
         def weigh_group_2(u):
             result = results.tile([P, F], F32)
-            nc.scalar.activation(out=result[:], in_=y_banks[u, 0][:], func=ACT.Copy, scale=weight[u][:, 0:1])
+            nc.scalar.activation(
+                out=result[:], in_=y_banks[GROUPS * u][:], func=ACT.Copy, scale=weight[u][:, 0:1]
+            )
             out_tiles[u] = result
 
         def add_group_1_and_store(u):
             b, i = u // Q_TILES, TILE_ORDER[u % Q_TILES]
             nc.vector.scalar_tensor_tensor(
                 out=out_tiles[u][:],
-                in0=y_banks[u, 1][:],
+                in0=y_banks[GROUPS * u + 1][:],
                 scalar=weight[u][:, 1:2],
                 in1=out_tiles[u][:],
                 op0=ALU.mult,
@@ -295,9 +305,9 @@ def tile_mixerdiffattention_pb_t_kernel(
             if live(t - GROUP_2_LAG):
                 weigh_group_2(t - GROUP_2_LAG)
             if live(t):
-                scores(2 * t + 1)
-                row_maximum(2 * t + 1)
-                numerators(2 * t)
+                scores(GROUPS * t + 1)
+                row_maximum(GROUPS * t + 1)
+                numerators(GROUPS * t)
             if live(t - GROUP_1_LAG):
                 add_group_1_and_store(t - GROUP_1_LAG)
             if live(t + INPUTS_AHEAD):
@@ -305,14 +315,14 @@ def tile_mixerdiffattention_pb_t_kernel(
             if live(t - TURN_LAG):
                 turn_e(t - TURN_LAG)
             if live(t + 1):
-                scores(2 * t + 2)
-                row_maximum(2 * t + 2)
+                scores(GROUPS * (t + 1))
+                row_maximum(GROUPS * (t + 1))
             if live(t):
-                numerators(2 * t + 1)
+                numerators(GROUPS * t + 1)
             if live(t - QUANTISE_LAG):
                 quantise_e(t - QUANTISE_LAG)
             if live(t - TURN_LAG):
-                weights(t - TURN_LAG)
+                invert_row_sums(t - TURN_LAG)
             if live(t + VALUES_AHEAD):
                 quantise_values(t + VALUES_AHEAD)
             if live(t - TURN_LAG):

@@ -36,6 +36,7 @@ INPUTS_AHEAD = Q_TILES
 VALUES_AHEAD = 2
 TURN_LAG = 1
 QUANTISE_LAG = 2
+WEIGHT_LAG = 2
 GROUP_2_LAG = 4
 GROUP_1_LAG = 5
 
@@ -57,6 +58,7 @@ def tile_mixerdiffattention_pb_t_kernel(
         grouped = ctx.enter_context(tc.tile_pool(name="grouped", bufs=QUANTISE_LAG - TURN_LAG + 2))
         quantised = ctx.enter_context(tc.tile_pool(name="quantised", bufs=GROUP_1_LAG - QUANTISE_LAG + 2))
         stats = ctx.enter_context(tc.tile_pool(name="stats", bufs=GROUP_1_LAG + 2))
+        pair_stats = ctx.enter_context(tc.tile_pool(name="pair_stats", bufs=(GROUP_1_LAG + 1) // 2 + 2))
         results = ctx.enter_context(tc.tile_pool(name="results", bufs=4))
         turned_psum = ctx.enter_context(tc.psum_pool(name="turned_psum", bufs=2))
         score_psum = ctx.enter_context(tc.psum_pool(name="score_psum", bufs=3))
@@ -211,25 +213,31 @@ def tile_mixerdiffattention_pb_t_kernel(
             u, place = divmod(h, GROUPS)
             i = TILE_ORDER[u % Q_TILES]
             n_keys = (i + 1) * P
-            if place == 0:
-                sums = stats.tile([P, GROUPS], F32)
-                row_sum[u] = sums
+            pair, member = divmod(u, 2)
+            if member == 0 and place == 0:
+                sums = pair_stats.tile([P, 2, GROUPS], F32)
+                row_sum[pair] = sums
             nc.scalar.activation(
                 out=e_fixed[i][:, place, :, : n_keys // PLANES].rearrange("p a (w c) -> p a w c", c=2),
                 in_=s_banks[h][:, :n_keys].rearrange("p (w a c) -> p a w c", a=PLANES, c=2),
                 func=ACT.Exp,
                 bias=neg_max[u][:, place : place + 1],
-                accum_out=row_sum[u][:, place : place + 1],
+                accum_out=row_sum[pair][:, member, place : place + 1],
             )
 
-        def invert_row_sums(u):
-            factors = stats.tile([P, GROUPS], F32)
-            nc.vector.reciprocal(out=factors[:], in_=row_sum[u][:])
-            weight[u] = factors
+        def invert_row_sums(pair):
+            factors = pair_stats.tile([P, 2, GROUPS], F32)
+            nc.vector.reciprocal(out=factors[:], in_=row_sum[pair][:])
+            weight[pair] = factors
 
-        def weight_group_2(u):
-            nc.vector.tensor_scalar_mul(
-                out=weight[u][:, 0:1], in0=weight[u][:, 0:1], scalar1=neg_lam[:, 0:1]
+        def weight_group_2(pair):
+            nc.gpsimd.tensor_scalar(
+                out=weight[pair][:, :, 0],
+                in0=weight[pair][:, :, 0],
+                scalar1=neg_lam[:, 0:1],
+                scalar2=0.0,
+                op0=ALU.mult,
+                op1=ALU.add,
             )
 
         def turn_e(u):
@@ -277,7 +285,7 @@ def tile_mixerdiffattention_pb_t_kernel(
         def weigh_group_2(u):
             result = results.tile([P, F], F32)
             nc.scalar.activation(
-                out=result[:], in_=y_banks[GROUPS * u][:], func=ACT.Copy, scale=weight[u][:, 0:1]
+                out=result[:], in_=y_banks[GROUPS * u][:], func=ACT.Copy, scale=weight[u // 2][:, u % 2, 0:1]
             )
             out_tiles[u] = result
 
@@ -286,7 +294,7 @@ def tile_mixerdiffattention_pb_t_kernel(
             nc.vector.scalar_tensor_tensor(
                 out=out_tiles[u][:],
                 in0=y_banks[GROUPS * u + 1][:],
-                scalar=weight[u][:, 1:2],
+                scalar=weight[u // 2][:, u % 2, 1:2],
                 in1=out_tiles[u][:],
                 op0=ALU.mult,
                 op1=ALU.add,
@@ -296,6 +304,8 @@ def tile_mixerdiffattention_pb_t_kernel(
         def step(t):
             if live(t + INPUTS_AHEAD) and (t + INPUTS_AHEAD) % Q_TILES == 0:
                 scale_queries((t + INPUTS_AHEAD) // Q_TILES)
+            if live(t - WEIGHT_LAG) and (t - WEIGHT_LAG) % 2 == 1:
+                weight_group_2((t - WEIGHT_LAG) // 2)
             if live(t + VALUES_AHEAD):
                 regroup_values(t + VALUES_AHEAD)
             if live(t - GROUP_2_LAG):
@@ -321,12 +331,10 @@ def tile_mixerdiffattention_pb_t_kernel(
                 numerators(GROUPS * t + 1)
             if live(t - QUANTISE_LAG):
                 quantise_e(t - QUANTISE_LAG)
-            if live(t - TURN_LAG):
-                invert_row_sums(t - TURN_LAG)
+            if live(t - TURN_LAG) and (t - TURN_LAG) % 2 == 1:
+                invert_row_sums((t - TURN_LAG) // 2)
             if live(t + VALUES_AHEAD):
                 quantise_values(t + VALUES_AHEAD)
-            if live(t - TURN_LAG):
-                weight_group_2(t - TURN_LAG)
 
         for t in range(-INPUTS_AHEAD, 0):
             step(t)

@@ -101,7 +101,7 @@ def tile_mixerdiffattention_pb_t_kernel(
             nc.sync.dma_start(out=k_sb[:], in_=k_rot[b].rearrange("(j p) h d -> p j (h d)", p=P))
             if b == 0:
                 for n, vec in enumerate((lambda_q1, lambda_q2, lambda_k1, lambda_k2)):
-                    nc.sync.dma_start(out=lam_in[:, n, :], in_=vec.partition_broadcast(P))
+                    nc.sync.dma_start(out=lam_in[0:1, n, :], in_=vec.rearrange("(o n) -> o n", o=1))
             v_sb = loads.tile([P, PACK, F], BF16, tag="v")
             nc.sync.dma_start(out=v_sb[:], in_=v[b].rearrange("(p t) o f -> p t (o f)", t=PACK))
             q_in.append(q_sb)
@@ -109,24 +109,34 @@ def tile_mixerdiffattention_pb_t_kernel(
             v_in.append(v_sb)
 
         neg_lam = const.tile([P, 1], F32)
+        lam_column = const.tile([P, 2], F32)
+        nc.vector.memset(lam_column[:], 0.0)
+        first_row = const.tile([P, P], F32)
+        nc.vector.memset(first_row[:], 0.0)
+        nc.vector.memset(first_row[0:1, :], 1.0)
 
         def compute_neg_lam():
             products = const.tile([P, 2, LAM_LEN], F32)
             nc.vector.tensor_tensor(
-                out=products[:], in0=lam_in[:, 0:2, :], in1=lam_in[:, 2:4, :], op=ALU.mult
+                out=products[0:1], in0=lam_in[0:1, 0:2, :], in1=lam_in[0:1, 2:4, :], op=ALU.mult
             )
             dots = const.tile([P, 2], F32)
-            nc.vector.reduce_sum(out=dots[:], in_=products[:], axis=AX.X)
+            nc.vector.reduce_sum(out=dots[0:1], in_=products[0:1], axis=AX.X)
             exp_dots = const.tile([P, 2], F32)
-            nc.scalar.activation(out=exp_dots[:], in_=dots[:], func=ACT.Exp)
+            nc.scalar.activation(out=exp_dots[0:1], in_=dots[0:1], func=ACT.Exp)
             nc.vector.tensor_scalar(
-                out=neg_lam[:],
-                in0=exp_dots[:, 1:2],
-                scalar1=exp_dots[:, 0:1],
+                out=lam_column[0:1, 0:1],
+                in0=exp_dots[0:1, 1:2],
+                scalar1=exp_dots[0:1, 0:1],
                 scalar2=-LAMBDA_INIT,
                 op0=ALU.subtract,
                 op1=ALU.add,
             )
+
+        def spread_neg_lam():
+            bank = turned_psum.tile([P, T], F32, tag="turned")
+            nc.tensor.matmul(bank[:, 0:2], lhsT=first_row[:], rhs=lam_column[:], start=True, stop=True)
+            nc.vector.tensor_copy(out=neg_lam[:], in_=bank[:, 0:1])
 
         qT, kT = {}, {}
         v_grouped, v_codes, v_scales = {}, {}, {}
@@ -340,4 +350,6 @@ def tile_mixerdiffattention_pb_t_kernel(
             step(t)
         compute_neg_lam()
         for t in range(0, UNITS + GROUP_1_LAG):
+            if t == WEIGHT_LAG:
+                spread_neg_lam()
             step(t)

@@ -33,7 +33,7 @@ HEAD_AT_PLACE = (1, 0)
 TILE_ORDER = (0, 3, 1, 2)
 
 INPUTS_AHEAD = Q_TILES
-VALUES_AHEAD = 2
+VALUES_AHEAD = 1
 TURN_LAG = 1
 QUANTISE_LAG = 2
 WEIGHT_LAG = 2
@@ -59,7 +59,7 @@ def tile_mixerdiffattention_pb_t_kernel(
         quantised = ctx.enter_context(tc.tile_pool(name="quantised", bufs=GROUP_1_LAG - QUANTISE_LAG + 2))
         stats = ctx.enter_context(tc.tile_pool(name="stats", bufs=GROUP_1_LAG + 2))
         pair_stats = ctx.enter_context(tc.tile_pool(name="pair_stats", bufs=(GROUP_1_LAG + 1) // 2 + 2))
-        results = ctx.enter_context(tc.tile_pool(name="results", bufs=4))
+        results = ctx.enter_context(tc.tile_pool(name="results", bufs=8))
         turned_psum = ctx.enter_context(tc.psum_pool(name="turned_psum", bufs=2))
         score_psum = ctx.enter_context(tc.psum_pool(name="score_psum", bufs=3))
         y_psum = ctx.enter_context(tc.psum_pool(name="y_psum", bufs=3))
@@ -80,7 +80,6 @@ def tile_mixerdiffattention_pb_t_kernel(
             channel_multiplier=1,
         )
         mask_bf16 = const.tile([P, P], BF16)
-        nc.vector.tensor_copy(out=mask_bf16[:], in_=mask_f32[:])
         zero_column = const.tile([P, 1], F32)
         nc.vector.memset(zero_column[:], 0.0)
         one_column = const.tile([P, 1], F32)
@@ -92,21 +91,41 @@ def tile_mixerdiffattention_pb_t_kernel(
             nc.vector.memset(e_tile[:], 0.0)
             e_fixed.append(e_tile)
 
-        q_in, k_in, v_in = [], [], []
+        q_heads, k_heads, q_tiles, v_in = [], [], [], []
         lam_in = const.tile([P, 4, LAM_LEN], BF16)
-        for b in range(B):
-            q_sb = loads.tile([P, Q_TILES, GROUPS * HD], BF16, tag="q")
-            nc.sync.dma_start(out=q_sb[:], in_=q_rot[b].rearrange("(j p) h d -> p j (h d)", p=P))
-            k_sb = loads.tile([P, Q_TILES, GROUPS * HD], BF16, tag="k")
-            nc.sync.dma_start(out=k_sb[:], in_=k_rot[b].rearrange("(j p) h d -> p j (h d)", p=P))
-            if b == 0:
-                for n, vec in enumerate((lambda_q1, lambda_q2, lambda_k1, lambda_k2)):
-                    nc.sync.dma_start(out=lam_in[0:1, n, :], in_=vec.rearrange("(o n) -> o n", o=1))
+
+        def load_first_entry():
+            first = {}
+            for head in HEAD_AT_PLACE:
+                for letter, source in (("k", k_rot), ("q", q_rot)):
+                    part = const.tile([P, Q_TILES, HD], BF16, name="first_%s%d" % (letter, head))
+                    nc.sync.dma_start(
+                        out=part[:], in_=source[0, :, head, :].rearrange("(j p) d -> p j d", p=P)
+                    )
+                    first[letter, head] = part[:]
+            q_heads.append([first["q", head] for head in range(GROUPS)])
+            k_heads.append([first["k", head] for head in range(GROUPS)])
+            q_tiles.append([first["q", head] for head in HEAD_AT_PLACE])
+
+        def load_both_heads(letter, source, b, heads):
+            both = loads.tile([P, Q_TILES, GROUPS * HD], BF16, tag=letter)
+            nc.sync.dma_start(out=both[:], in_=source[b].rearrange("(j p) h d -> p j (h d)", p=P))
+            heads.append([both[:, :, head * HD : (head + 1) * HD] for head in range(GROUPS)])
+            return both
+
+        def load_values(b):
             v_sb = loads.tile([P, PACK, F], BF16, tag="v")
             nc.sync.dma_start(out=v_sb[:], in_=v[b].rearrange("(p t) o f -> p t (o f)", t=PACK))
-            q_in.append(q_sb)
-            k_in.append(k_sb)
             v_in.append(v_sb)
+
+        load_first_entry()
+        for n, vec in enumerate((lambda_q1, lambda_q2, lambda_k1, lambda_k2)):
+            nc.sync.dma_start(out=lam_in[0:1, n, :], in_=vec.rearrange("(o n) -> o n", o=1))
+        for b in range(1, B):
+            load_both_heads("k", k_rot, b, k_heads)
+            load_values(b - 1)
+            q_tiles.append([load_both_heads("q", q_rot, b, q_heads)[:]])
+        load_values(B - 1)
 
         neg_lam = const.tile([P, 1], F32)
         lam_column = const.tile([P, 2], F32)
@@ -148,21 +167,17 @@ def tile_mixerdiffattention_pb_t_kernel(
             return 0 <= u < UNITS
 
         def scale_queries(b):
-            nc.vector.tensor_scalar_mul(out=q_in[b][:], in0=q_in[b][:], scalar1=SCORE_SCALE)
+            for whole in q_tiles[b]:
+                nc.vector.tensor_scalar_mul(out=whole, in0=whole, scalar1=SCORE_SCALE)
 
         def turn_input(u):
             b, quarter = divmod(u, Q_TILES)
             place = quarter // 2
-            source, turned = ((k_in, kT), (q_in, qT))[quarter % 2]
-            words = source[b][:].bitcast(F32)
-            head = HEAD_AT_PLACE[place]
+            source, turned = ((k_heads, kT), (q_heads, qT))[quarter % 2]
+            words = source[b][HEAD_AT_PLACE[place]].bitcast(F32)
             bank = turned_psum.tile([P, T], F32, tag="turned")
             for j in range(Q_TILES):
-                nc.tensor.transpose(
-                    bank[:, j * P : (j + 1) * P],
-                    words[:, j, head * PAIRS : (head + 1) * PAIRS],
-                    ident_f32[:],
-                )
+                nc.tensor.transpose(bank[:, j * P : (j + 1) * P], words[:, j, :], ident_f32[:])
             rows = turned_inputs.tile([P, T, 2], BF16, tag="turned%d" % (quarter % 2))
             nc.scalar.copy(out=rows[:].bitcast(F32).rearrange("p r w -> p (r w)"), in_=bank[:])
             turned[b, place] = rows
@@ -312,7 +327,7 @@ def tile_mixerdiffattention_pb_t_kernel(
             nc.sync.dma_start(out=out[b, i * P : (i + 1) * P, :], in_=out_tiles[u][:])
 
         def step(t):
-            if live(t + INPUTS_AHEAD) and (t + INPUTS_AHEAD) % Q_TILES == 0:
+            if 0 < t + INPUTS_AHEAD < UNITS and (t + INPUTS_AHEAD) % Q_TILES == 0:
                 scale_queries((t + INPUTS_AHEAD) // Q_TILES)
             if live(t - WEIGHT_LAG) and (t - WEIGHT_LAG) % 2 == 1:
                 weight_group_2((t - WEIGHT_LAG) // 2)
@@ -346,6 +361,8 @@ def tile_mixerdiffattention_pb_t_kernel(
             if live(t + VALUES_AHEAD):
                 quantise_values(t + VALUES_AHEAD)
 
+        scale_queries(0)
+        nc.vector.tensor_copy(out=mask_bf16[:], in_=mask_f32[:])
         for t in range(-INPUTS_AHEAD, 0):
             step(t)
         compute_neg_lam()

@@ -34,11 +34,12 @@ TILE_ORDER = (0, 3, 1, 2)
 
 INPUTS_AHEAD = Q_TILES
 VALUES_AHEAD = 1
-TURN_LAG = 1
-QUANTISE_LAG = 2
+TURN_LAG = 2
+QUANTISE_LAG = 3
+INVERT_LAG = 1
 WEIGHT_LAG = 2
-GROUP_2_LAG = 4
-GROUP_1_LAG = 5
+GROUP_2_LAG = 5
+GROUP_1_LAG = 6
 
 FLOPS = B * GROUPS * (2 * T * T * HD + 2 * T * T * F)
 
@@ -166,6 +167,11 @@ def tile_mixerdiffattention_pb_t_kernel(
         def live(u):
             return 0 <= u < UNITS
 
+        def half_unit(h):
+            turn, second = divmod(h, 2)
+            two_units, place = divmod(turn, GROUPS)
+            return 2 * two_units + second, place
+
         def scale_queries(b):
             for whole in q_tiles[b]:
                 nc.vector.tensor_scalar_mul(out=whole, in0=whole, scalar1=SCORE_SCALE)
@@ -209,7 +215,7 @@ def tile_mixerdiffattention_pb_t_kernel(
             )
 
         def scores(h):
-            u, place = divmod(h, GROUPS)
+            u, place = half_unit(h)
             b, i = u // Q_TILES, TILE_ORDER[u % Q_TILES]
             rows = slice(i * P, (i + 1) * P)
             n_keys = (i + 1) * P
@@ -225,7 +231,7 @@ def tile_mixerdiffattention_pb_t_kernel(
             s_banks[h] = bank
 
         def row_maximum(h):
-            u, place = divmod(h, GROUPS)
+            u, place = half_unit(h)
             n_keys = (TILE_ORDER[u % Q_TILES] + 1) * P
             if place == 0:
                 maxima = stats.tile([P, GROUPS], F32)
@@ -235,7 +241,7 @@ def tile_mixerdiffattention_pb_t_kernel(
             )
 
         def numerators(h):
-            u, place = divmod(h, GROUPS)
+            u, place = half_unit(h)
             i = TILE_ORDER[u % Q_TILES]
             n_keys = (i + 1) * P
             pair, member = divmod(u, 2)
@@ -356,8 +362,8 @@ def tile_mixerdiffattention_pb_t_kernel(
                 numerators(GROUPS * t + 1)
             if live(t - QUANTISE_LAG):
                 quantise_e(t - QUANTISE_LAG)
-            if live(t - TURN_LAG) and (t - TURN_LAG) % 2 == 1:
-                invert_row_sums((t - TURN_LAG) // 2)
+            if live(t - INVERT_LAG) and (t - INVERT_LAG) % 2 == 1:
+                invert_row_sums((t - INVERT_LAG) // 2)
             if live(t + VALUES_AHEAD):
                 quantise_values(t + VALUES_AHEAD)
 

@@ -92,7 +92,7 @@ def tile_mixerdiffattention_pb_t_kernel(
             nc.vector.memset(e_tile[:], 0.0)
             e_fixed.append(e_tile)
 
-        q_heads, k_heads, q_tiles, v_in = [], [], [], []
+        q_heads, k_heads, v_in = [], [], []
         lam_in = const.tile([P, 4, LAM_LEN], BF16)
 
         def load_first_entry():
@@ -106,13 +106,11 @@ def tile_mixerdiffattention_pb_t_kernel(
                     first[letter, head] = part[:]
             q_heads.append([first["q", head] for head in range(GROUPS)])
             k_heads.append([first["k", head] for head in range(GROUPS)])
-            q_tiles.append([first["q", head] for head in HEAD_AT_PLACE])
 
         def load_both_heads(letter, source, b, heads):
             both = loads.tile([P, Q_TILES, GROUPS * HD], BF16, tag=letter)
             nc.sync.dma_start(out=both[:], in_=source[b].rearrange("(j p) h d -> p j (h d)", p=P))
             heads.append([both[:, :, head * HD : (head + 1) * HD] for head in range(GROUPS)])
-            return both
 
         def load_values(b):
             v_sb = loads.tile([P, PACK, F], BF16, tag="v")
@@ -125,7 +123,7 @@ def tile_mixerdiffattention_pb_t_kernel(
         for b in range(1, B):
             load_both_heads("k", k_rot, b, k_heads)
             load_values(b - 1)
-            q_tiles.append([load_both_heads("q", q_rot, b, q_heads)[:]])
+            load_both_heads("q", q_rot, b, q_heads)
         load_values(B - 1)
 
         neg_lam = const.tile([P, 1], F32)
@@ -172,10 +170,6 @@ def tile_mixerdiffattention_pb_t_kernel(
             two_units, place = divmod(turn, GROUPS)
             return 2 * two_units + second, place
 
-        def scale_queries(b):
-            for whole in q_tiles[b]:
-                nc.vector.tensor_scalar_mul(out=whole, in0=whole, scalar1=SCORE_SCALE)
-
         def turn_input(u):
             b, quarter = divmod(u, Q_TILES)
             place = quarter // 2
@@ -185,7 +179,12 @@ def tile_mixerdiffattention_pb_t_kernel(
             for j in range(Q_TILES):
                 nc.tensor.transpose(bank[:, j * P : (j + 1) * P], words[:, j, :], ident_f32[:])
             rows = turned_inputs.tile([P, T, 2], BF16, tag="turned%d" % (quarter % 2))
-            nc.scalar.copy(out=rows[:].bitcast(F32).rearrange("p r w -> p (r w)"), in_=bank[:])
+            if quarter % 2 == 0:
+                nc.scalar.copy(out=rows[:].bitcast(F32).rearrange("p r w -> p (r w)"), in_=bank[:])
+            else:
+                nc.vector.tensor_scalar_mul(
+                    out=rows[:].rearrange("p r w -> p (r w)"), in0=bank[:].bitcast(BF16), scalar1=SCORE_SCALE
+                )
             turned[b, place] = rows
 
         def regroup_values(u):
@@ -281,8 +280,7 @@ def tile_mixerdiffattention_pb_t_kernel(
                         bank[:, column : column + P], e_words[:, place, plane, :], ident_f32[:]
                     )
             keys_together = grouped.tile([P, GROUPS * P, PACK], BF16, align_bytes=64)
-            copy = nc.vector.tensor_copy if u % 2 == 0 else nc.scalar.copy
-            copy(
+            nc.scalar.copy(
                 out=keys_together[:].bitcast(F32).rearrange("p (n r) a -> p n r a", n=GROUPS),
                 in_=bank[:].rearrange("p (n a r) -> p n r a", n=GROUPS, a=PLANES),
             )
@@ -333,8 +331,6 @@ def tile_mixerdiffattention_pb_t_kernel(
             nc.sync.dma_start(out=out[b, i * P : (i + 1) * P, :], in_=out_tiles[u][:])
 
         def step(t):
-            if 0 < t + INPUTS_AHEAD < UNITS and (t + INPUTS_AHEAD) % Q_TILES == 0:
-                scale_queries((t + INPUTS_AHEAD) // Q_TILES)
             if live(t - WEIGHT_LAG) and (t - WEIGHT_LAG) % 2 == 1:
                 weight_group_2((t - WEIGHT_LAG) // 2)
             if live(t + VALUES_AHEAD):
@@ -367,7 +363,6 @@ def tile_mixerdiffattention_pb_t_kernel(
             if live(t + VALUES_AHEAD):
                 quantise_values(t + VALUES_AHEAD)
 
-        scale_queries(0)
         nc.vector.tensor_copy(out=mask_bf16[:], in_=mask_f32[:])
         for t in range(-INPUTS_AHEAD, 0):
             step(t)

@@ -41,6 +41,8 @@ WEIGHT_LAG = 2
 GROUP_2_LAG = 5
 GROUP_1_LAG = 6
 
+VECTOR_TURNS_EVERY = 8
+
 FLOPS = B * GROUPS * (2 * T * T * HD + 2 * T * T * F)
 
 
@@ -61,9 +63,7 @@ def tile_mixerdiffattention_pb_t_kernel(
         stats = ctx.enter_context(tc.tile_pool(name="stats", bufs=GROUP_1_LAG + 2))
         pair_stats = ctx.enter_context(tc.tile_pool(name="pair_stats", bufs=(GROUP_1_LAG + 1) // 2 + 2))
         results = ctx.enter_context(tc.tile_pool(name="results", bufs=8))
-        turned_psum = ctx.enter_context(tc.psum_pool(name="turned_psum", bufs=2))
-        score_psum = ctx.enter_context(tc.psum_pool(name="score_psum", bufs=3))
-        y_psum = ctx.enter_context(tc.psum_pool(name="y_psum", bufs=3))
+        psum = ctx.enter_context(tc.psum_pool(name="psum", bufs=8))
 
         ident_f32 = const.tile([P, P], F32)
         make_identity(nc, ident_f32[:])
@@ -152,7 +152,7 @@ def tile_mixerdiffattention_pb_t_kernel(
             )
 
         def spread_neg_lam():
-            bank = turned_psum.tile([P, T], F32, tag="turned")
+            bank = psum.tile([P, T], F32, tag="bank")
             nc.tensor.matmul(bank[:, 0:2], lhsT=first_row[:], rhs=lam_column[:], start=True, stop=True)
             nc.vector.tensor_copy(out=neg_lam[:], in_=bank[:, 0:1])
 
@@ -175,7 +175,7 @@ def tile_mixerdiffattention_pb_t_kernel(
             place = quarter // 2
             source, turned = ((k_heads, kT), (q_heads, qT))[quarter % 2]
             words = source[b][HEAD_AT_PLACE[place]].bitcast(F32)
-            bank = turned_psum.tile([P, T], F32, tag="turned")
+            bank = psum.tile([P, T], F32, tag="bank")
             for j in range(Q_TILES):
                 nc.tensor.transpose(bank[:, j * P : (j + 1) * P], words[:, j, :], ident_f32[:])
             rows = turned_inputs.tile([P, T, 2], BF16, tag="turned%d" % (quarter % 2))
@@ -219,7 +219,7 @@ def tile_mixerdiffattention_pb_t_kernel(
             rows = slice(i * P, (i + 1) * P)
             n_keys = (i + 1) * P
             queries, keys = qT[b, place], kT[b, place]
-            bank = score_psum.tile([P, T], F32, tag="scores")
+            bank = psum.tile([P, T], F32, tag="bank")
             nc.tensor.matmul(
                 bank[:, :n_keys], lhsT=queries[:, rows, 0], rhs=keys[:, :n_keys, 0], start=True, stop=False
             )
@@ -272,7 +272,7 @@ def tile_mixerdiffattention_pb_t_kernel(
 
         def turn_e(u):
             e_words = e_fixed[TILE_ORDER[u % Q_TILES]][:].bitcast(F32)
-            bank = turned_psum.tile([P, T], F32, tag="turned")
+            bank = psum.tile([P, T], F32, tag="bank")
             for place in range(GROUPS):
                 for plane in range(PLANES):
                     column = (PLANES * place + plane) * P
@@ -280,7 +280,8 @@ def tile_mixerdiffattention_pb_t_kernel(
                         bank[:, column : column + P], e_words[:, place, plane, :], ident_f32[:]
                     )
             keys_together = grouped.tile([P, GROUPS * P, PACK], BF16, align_bytes=64)
-            nc.scalar.copy(
+            copy = nc.vector.tensor_copy if u % VECTOR_TURNS_EVERY == 0 else nc.scalar.copy
+            copy(
                 out=keys_together[:].bitcast(F32).rearrange("p (n r) a -> p n r a", n=GROUPS),
                 in_=bank[:].rearrange("p (n a r) -> p n r a", n=GROUPS, a=PLANES),
             )
@@ -299,7 +300,7 @@ def tile_mixerdiffattention_pb_t_kernel(
         def product(u, place):
             b = u // Q_TILES
             queries = slice(place * P, (place + 1) * P)
-            bank = y_psum.tile([P, F], F32, tag="y")
+            bank = psum.tile([P, F], F32, tag="bank")
             nc.tensor.matmul_mx(
                 out=bank[:],
                 lhsT=e_codes[u][:, queries].bitcast(FP8X4),

@@ -7,6 +7,7 @@ from concourse.masks import make_identity
 F32 = mybir.dt.float32
 BF16 = mybir.dt.bfloat16
 U32 = mybir.dt.uint32
+I32 = mybir.dt.int32
 U8 = mybir.dt.uint8
 FP8X4 = mybir.dt.float8_e4m3fn_x4
 ALU = mybir.AluOpType
@@ -31,17 +32,20 @@ MASKED = -1.0e30
 UNITS = B * Q_TILES
 HEAD_AT_PLACE = (1, 0)
 TILE_ORDER = (0, 3, 1, 2)
+PRODUCT_ORDER = (3, 1, 2, 0)
+KEYS_OF_3, KEYS_OF_20, KEYS_OF_1 = "tile 3", "tiles 2 and 0", "tile 1"
+WORDS = T // PACK
+SCALE_WORDS = F // PACK
+V_WORDS = F + SCALE_WORDS
 
 INPUTS_AHEAD = Q_TILES
 VALUES_AHEAD = 1
-TURN_LAG = 2
-QUANTISE_LAG = 3
 INVERT_LAG = 1
 WEIGHT_LAG = 2
-GROUP_2_LAG = 5
-GROUP_1_LAG = 6
-
-VECTOR_TURNS_EVERY = 8
+GROUP_2_LAG = 6
+GROUP_1_LAG = 7
+MOVE_LAG = 3
+LOADS_AT_ONCE = 6
 
 FLOPS = B * GROUPS * (2 * T * T * HD + 2 * T * T * F)
 
@@ -57,11 +61,11 @@ def tile_mixerdiffattention_pb_t_kernel(
         loads = ctx.enter_context(tc.tile_pool(name="loads", bufs=B))
         turned_inputs = ctx.enter_context(tc.tile_pool(name="turned_inputs", bufs=2 * GROUPS))
         regrouped = ctx.enter_context(tc.tile_pool(name="regrouped", bufs=1))
-        values = ctx.enter_context(tc.tile_pool(name="values", bufs=3))
-        grouped = ctx.enter_context(tc.tile_pool(name="grouped", bufs=QUANTISE_LAG - TURN_LAG + 2))
-        quantised = ctx.enter_context(tc.tile_pool(name="quantised", bufs=GROUP_1_LAG - QUANTISE_LAG + 2))
+        stacks = ctx.enter_context(tc.tile_pool(name="stacks", bufs=2))
+        grouped = ctx.enter_context(tc.tile_pool(name="grouped", bufs=2))
+        quantised = ctx.enter_context(tc.tile_pool(name="quantised", bufs=2))
         stats = ctx.enter_context(tc.tile_pool(name="stats", bufs=GROUP_1_LAG + 2))
-        pair_stats = ctx.enter_context(tc.tile_pool(name="pair_stats", bufs=(GROUP_1_LAG + 1) // 2 + 2))
+        pair_stats = ctx.enter_context(tc.tile_pool(name="pair_stats", bufs=8))
         results = ctx.enter_context(tc.tile_pool(name="results", bufs=8))
         psum = ctx.enter_context(tc.psum_pool(name="psum", bufs=8))
 
@@ -86,11 +90,22 @@ def tile_mixerdiffattention_pb_t_kernel(
         one_column = const.tile([P, 1], F32)
         nc.scalar.activation(out=one_column[:], in_=zero_column[:], func=ACT.Exp)
 
-        e_fixed = []
-        for i in range(Q_TILES):
-            e_tile = const.tile([P, GROUPS, PLANES, T // PLANES], BF16, name="e_tile%d" % i)
-            nc.vector.memset(e_tile[:], 0.0)
-            e_fixed.append(e_tile)
+        def value_tiles(name, count):
+            tiles = []
+            for n in range(count):
+                v_tile = const.tile([P, V_WORDS], U32, name="%s_%d" % (name, n), align_bytes=64)
+                tiles.append(v_tile)
+            return tiles
+
+        v_whole = value_tiles("v_whole", 3)
+        v_part = {}
+        for key in ((2, 0), (0, 0), (1, 0), (1, 1)):
+            v_part[key] = value_tiles("v_part_%d_%d" % key, 2)
+        for v_tile in v_whole:
+            nc.vector.memset(v_tile[:, F:].bitcast(I32), 0)
+        for tiles in v_part.values():
+            for v_tile in tiles:
+                nc.vector.memset(v_tile[:].bitcast(I32), 0)
 
         q_heads, k_heads, v_in = [], [], []
         lam_in = const.tile([P, 4, LAM_LEN], BF16)
@@ -120,11 +135,22 @@ def tile_mixerdiffattention_pb_t_kernel(
         load_first_entry()
         for n, vec in enumerate((lambda_q1, lambda_q2, lambda_k1, lambda_k2)):
             nc.sync.dma_start(out=lam_in[0:1, n, :], in_=vec.rearrange("(o n) -> o n", o=1))
+        later_loads = []
         for b in range(1, B):
-            load_both_heads("k", k_rot, b, k_heads)
-            load_values(b - 1)
-            load_both_heads("q", q_rot, b, q_heads)
-        load_values(B - 1)
+            later_loads += [("k", b), ("v", b - 1), ("q", b)]
+        later_loads.append(("v", B - 1))
+
+        def load(n):
+            letter, b = later_loads[n]
+            if letter == "v":
+                load_values(b)
+            elif letter == "k":
+                load_both_heads("k", k_rot, b, k_heads)
+            else:
+                load_both_heads("q", q_rot, b, q_heads)
+
+        for n in range(LOADS_AT_ONCE):
+            load(n)
 
         neg_lam = const.tile([P, 1], F32)
         lam_column = const.tile([P, 2], F32)
@@ -157,7 +183,8 @@ def tile_mixerdiffattention_pb_t_kernel(
             nc.vector.tensor_copy(out=neg_lam[:], in_=bank[:, 0:1])
 
         qT, kT = {}, {}
-        v_grouped, v_codes, v_scales = {}, {}, {}
+        v_grouped = {}
+        e_stack = {}
         s_banks, neg_max, row_sum, weight = {}, {}, {}, {}
         e_grouped, e_codes, e_scales = {}, {}, {}
         y_banks, out_tiles = {}, {}
@@ -202,16 +229,23 @@ def tile_mixerdiffattention_pb_t_kernel(
 
         def quantise_values(u):
             b, quarter = divmod(u, Q_TILES)
-            if quarter == 0:
-                codes = values.tile([P, F], U32, align_bytes=64)
-                scales = values.tile([P, F], U8, align_bytes=64)
-                v_codes[b], v_scales[b] = codes, scales
             features = slice(quarter * P, (quarter + 1) * P)
+            v_tile = v_whole[b % len(v_whole)]
             nc.vector.quantize_mx(
-                out=v_codes[b][:, features].bitcast(FP8X4),
-                scales=v_scales[b][:, features],
+                out=v_tile[:, features].bitcast(FP8X4),
+                scales=v_tile[:, F:].bitcast(U8)[:, features],
                 in_=v_grouped[u][:].rearrange("p f t -> p (f t)"),
             )
+
+        def move_values(b):
+            whole = v_whole[b % len(v_whole)]
+            for (i, place), tiles in v_part.items():
+                rows = (i + 1) * P // PACK
+                first = {2: 0, 0: WORDS - rows, 1: place * rows}[i]
+                nc.sync.dma_start(
+                    out=tiles[b % len(tiles)][first : first + rows, :].bitcast(I32),
+                    in_=whole[0:rows, :].bitcast(I32),
+                )
 
         def scores(h):
             u, place = half_unit(h)
@@ -241,14 +275,22 @@ def tile_mixerdiffattention_pb_t_kernel(
 
         def numerators(h):
             u, place = half_unit(h)
-            i = TILE_ORDER[u % Q_TILES]
+            b, i = u // Q_TILES, TILE_ORDER[u % Q_TILES]
             n_keys = (i + 1) * P
             pair, member = divmod(u, 2)
             if member == 0 and place == 0:
                 sums = pair_stats.tile([P, 2, GROUPS], F32)
                 row_sum[pair] = sums
+            stack = {3: KEYS_OF_3, 2: KEYS_OF_20, 0: KEYS_OF_20, 1: KEYS_OF_1}[i]
+            if (b, stack) not in e_stack:
+                width = 1 if stack == KEYS_OF_1 else GROUPS
+                e_tile = stacks.tile([P, width, PLANES, T // PLANES], BF16, name="e_" + stack.replace(" ", "_"))
+                e_stack[b, stack] = e_tile
+            half = n_keys // PLANES
+            first = {3: 0, 2: 0, 0: T // PLANES - half, 1: place * half}[i]
+            e_out = e_stack[b, stack][:, 0 if i == 1 else place, :, first : first + half]
             nc.scalar.activation(
-                out=e_fixed[i][:, place, :, : n_keys // PLANES].rearrange("p a (w c) -> p a w c", c=2),
+                out=e_out.rearrange("p a (w c) -> p a w c", c=2),
                 in_=s_banks[h][:, :n_keys].rearrange("p (w a c) -> p a w c", a=PLANES, c=2),
                 func=ACT.Exp,
                 bias=neg_max[u][:, place : place + 1],
@@ -270,66 +312,83 @@ def tile_mixerdiffattention_pb_t_kernel(
                 op1=ALU.add,
             )
 
-        def turn_e(u):
-            e_words = e_fixed[TILE_ORDER[u % Q_TILES]][:].bitcast(F32)
+        def turn_e(b, stack, first, count):
+            e_words = e_stack[b, stack][:].bitcast(F32)
+            width = e_words.shape[1]
             bank = psum.tile([P, T], F32, tag="bank")
-            for place in range(GROUPS):
+            for n in range(count):
                 for plane in range(PLANES):
-                    column = (PLANES * place + plane) * P
+                    column = (PLANES * n + plane) * P
                     nc.tensor.transpose(
-                        bank[:, column : column + P], e_words[:, place, plane, :], ident_f32[:]
+                        bank[:, column : column + P], e_words[:, first + n, plane, :], ident_f32[:]
                     )
-            keys_together = grouped.tile([P, GROUPS * P, PACK], BF16, align_bytes=64)
-            copy = nc.vector.tensor_copy if u % VECTOR_TURNS_EVERY == 0 else nc.scalar.copy
-            copy(
-                out=keys_together[:].bitcast(F32).rearrange("p (n r) a -> p n r a", n=GROUPS),
-                in_=bank[:].rearrange("p (n a r) -> p n r a", n=GROUPS, a=PLANES),
+            if first == 0:
+                keys_together = grouped.tile(
+                    [P, width * P, PACK], BF16, align_bytes=64, name="grouped_" + stack.replace(" ", "_")
+                )
+                e_grouped[b, stack] = keys_together
+            nc.scalar.copy(
+                out=e_grouped[b, stack][:]
+                .bitcast(F32)[:, first * P : (first + count) * P, :]
+                .rearrange("p (n r) a -> p n r a", n=count),
+                in_=bank[:, : count * PLANES * P].rearrange("p (n a r) -> p n r a", n=count, a=PLANES),
             )
-            e_grouped[u] = keys_together
 
-        def quantise_e(u):
-            codes = quantised.tile([P, GROUPS * P], U32, align_bytes=64)
-            scales = quantised.tile([P, GROUPS * P], U8, align_bytes=64)
+        def quantise_e(b, stack):
+            name = stack.replace(" ", "_")
+            columns = e_grouped[b, stack].shape[1]
+            codes = quantised.tile([P, columns], U32, align_bytes=64, name="codes_" + name)
+            scales = quantised.tile([P, columns], U8, align_bytes=64, name="scales_" + name)
             nc.vector.quantize_mx(
                 out=codes[:].bitcast(FP8X4),
                 scales=scales[:],
-                in_=e_grouped[u][:].rearrange("p r t -> p (r t)"),
+                in_=e_grouped[b, stack][:].rearrange("p r t -> p (r t)"),
             )
-            e_codes[u], e_scales[u] = codes, scales
+            e_codes[b, stack], e_scales[b, stack] = codes, scales
 
-        def product(u, place):
-            b = u // Q_TILES
-            queries = slice(place * P, (place + 1) * P)
+        def product_unit(n):
+            b, i = n // Q_TILES, PRODUCT_ORDER[n % Q_TILES]
+            pair, member = divmod(b * Q_TILES + TILE_ORDER.index(i), 2)
+            return b, i, pair, member
+
+        def product(n, place):
+            b, i, pair, member = product_unit(n)
+            stack = {3: KEYS_OF_3, 2: KEYS_OF_20, 0: KEYS_OF_20, 1: KEYS_OF_1}[i]
+            column = 0 if i == 1 else place * P
+            queries = slice(column, column + P)
+            v_tiles = v_whole if i == 3 else v_part[i, place if i == 1 else 0]
+            v_tile = v_tiles[b % len(v_tiles)]
             bank = psum.tile([P, F], F32, tag="bank")
             nc.tensor.matmul_mx(
                 out=bank[:],
-                lhsT=e_codes[u][:, queries].bitcast(FP8X4),
-                lhsT_scale=e_scales[u][:, queries],
-                rhs=v_codes[b][:].bitcast(FP8X4),
-                rhs_scale=v_scales[b][:],
+                lhsT=e_codes[b, stack][:, queries].bitcast(FP8X4),
+                lhsT_scale=e_scales[b, stack][:, queries],
+                rhs=v_tile[:, :F].bitcast(FP8X4),
+                rhs_scale=v_tile[:, F:].bitcast(U8),
                 start=True,
                 stop=True,
             )
-            y_banks[GROUPS * u + place] = bank
+            y_banks[GROUPS * n + place] = bank
 
-        def weigh_group_2(u):
+        def weigh_group_2(n):
+            b, i, pair, member = product_unit(n)
             result = results.tile([P, F], F32)
             nc.scalar.activation(
-                out=result[:], in_=y_banks[GROUPS * u][:], func=ACT.Copy, scale=weight[u // 2][:, u % 2, 0:1]
+                out=result[:], in_=y_banks[GROUPS * n][:], func=ACT.Copy, scale=weight[pair][:, member, 0:1]
             )
-            out_tiles[u] = result
+            out_tiles[n] = result
 
-        def add_group_1_and_store(u):
-            b, i = u // Q_TILES, TILE_ORDER[u % Q_TILES]
+        def add_group_1_and_store(n):
+            b, i, pair, member = product_unit(n)
             nc.vector.scalar_tensor_tensor(
-                out=out_tiles[u][:],
-                in0=y_banks[GROUPS * u + 1][:],
-                scalar=weight[u // 2][:, u % 2, 1:2],
-                in1=out_tiles[u][:],
+                out=out_tiles[n][:],
+                in0=y_banks[GROUPS * n + 1][:],
+                scalar=weight[pair][:, member, 1:2],
+                in1=out_tiles[n][:],
                 op0=ALU.mult,
                 op1=ALU.add,
             )
-            nc.sync.dma_start(out=out[b, i * P : (i + 1) * P, :], in_=out_tiles[u][:])
+            nc.sync.dma_start(out=out[b, i * P : (i + 1) * P, :], in_=out_tiles[n][:])
 
         def step(t):
             if live(t - WEIGHT_LAG) and (t - WEIGHT_LAG) % 2 == 1:
@@ -348,17 +407,23 @@ def tile_mixerdiffattention_pb_t_kernel(
                 numerators(GROUPS * t)
             if live(t - GROUP_1_LAG):
                 add_group_1_and_store(t - GROUP_1_LAG)
+            if live(t - MOVE_LAG) and (t - MOVE_LAG) % Q_TILES == 0:
+                move_values((t - MOVE_LAG) // Q_TILES)
+            if live(t) and LOADS_AT_ONCE + t < len(later_loads):
+                load(LOADS_AT_ONCE + t)
             if live(t + INPUTS_AHEAD):
                 turn_input(t + INPUTS_AHEAD)
-            if live(t - TURN_LAG):
-                turn_e(t - TURN_LAG)
+            if live(t - 2):
+                b, turn = divmod(t - 2, Q_TILES)
+                turn_e(b, *((KEYS_OF_3, 0, 1), (KEYS_OF_3, 1, 1), (KEYS_OF_1, 0, 1), (KEYS_OF_20, 0, 2))[turn])
             if live(t + 1):
                 scores(GROUPS * (t + 1))
                 row_maximum(GROUPS * (t + 1))
             if live(t):
                 numerators(GROUPS * t + 1)
-            if live(t - QUANTISE_LAG):
-                quantise_e(t - QUANTISE_LAG)
+            if live(t - 4) and (t - 4) % Q_TILES < 3:
+                b, turn = divmod(t - 4, Q_TILES)
+                quantise_e(b, (KEYS_OF_3, KEYS_OF_1, KEYS_OF_20)[turn])
             if live(t - INVERT_LAG) and (t - INVERT_LAG) % 2 == 1:
                 invert_row_sums((t - INVERT_LAG) // 2)
             if live(t + VALUES_AHEAD):

@@ -39,13 +39,13 @@ SCALE_WORDS = F // PACK
 V_WORDS = F + SCALE_WORDS
 
 INPUTS_AHEAD = Q_TILES
-VALUES_AHEAD = 1
+VALUE_BUFFERS = 4
+PART_BUFFERS = 3
 INVERT_LAG = 1
 WEIGHT_LAG = 2
 GROUP_2_LAG = 6
 GROUP_1_LAG = 7
-MOVE_LAG = 3
-LOADS_AT_ONCE = 6
+LOADS_AT_ONCE = 7
 
 FLOPS = B * GROUPS * (2 * T * T * HD + 2 * T * T * F)
 
@@ -60,7 +60,7 @@ def tile_mixerdiffattention_pb_t_kernel(
         const = ctx.enter_context(tc.tile_pool(name="const", bufs=1))
         loads = ctx.enter_context(tc.tile_pool(name="loads", bufs=B))
         turned_inputs = ctx.enter_context(tc.tile_pool(name="turned_inputs", bufs=2 * GROUPS))
-        regrouped = ctx.enter_context(tc.tile_pool(name="regrouped", bufs=1))
+        regrouped = ctx.enter_context(tc.tile_pool(name="regrouped", bufs=2))
         stacks = ctx.enter_context(tc.tile_pool(name="stacks", bufs=2))
         grouped = ctx.enter_context(tc.tile_pool(name="grouped", bufs=2))
         quantised = ctx.enter_context(tc.tile_pool(name="quantised", bufs=2))
@@ -97,15 +97,18 @@ def tile_mixerdiffattention_pb_t_kernel(
                 tiles.append(v_tile)
             return tiles
 
-        v_whole = value_tiles("v_whole", 3)
+        v_whole = value_tiles("v_whole", VALUE_BUFFERS)
         v_part = {}
         for key in ((2, 0), (0, 0), (1, 0), (1, 1)):
-            v_part[key] = value_tiles("v_part_%d_%d" % key, 2)
+            v_part[key] = value_tiles("v_part_%d_%d" % key, PART_BUFFERS)
         for v_tile in v_whole:
             nc.vector.memset(v_tile[:, F:].bitcast(I32), 0)
-        for tiles in v_part.values():
-            for v_tile in tiles:
-                nc.vector.memset(v_tile[:].bitcast(I32), 0)
+
+        def clear_parts(n):
+            for tiles in v_part.values():
+                nc.vector.memset(tiles[n][:].bitcast(I32), 0)
+
+        clear_parts(0)
 
         q_heads, k_heads, v_in = [], [], []
         lam_in = const.tile([P, 4, LAM_LEN], BF16)
@@ -137,8 +140,8 @@ def tile_mixerdiffattention_pb_t_kernel(
             nc.sync.dma_start(out=lam_in[0:1, n, :], in_=vec.rearrange("(o n) -> o n", o=1))
         later_loads = []
         for b in range(1, B):
-            later_loads += [("k", b), ("v", b - 1), ("q", b)]
-        later_loads.append(("v", B - 1))
+            later_loads += [("k", b), ("q", b), ("v", b)]
+        later_loads = [("k", 1), ("v", 0), ("q", 1), ("v", 1)] + later_loads[3:]
 
         def load(n):
             letter, b = later_loads[n]
@@ -390,11 +393,18 @@ def tile_mixerdiffattention_pb_t_kernel(
             )
             nc.sync.dma_start(out=out[b, i * P : (i + 1) * P, :], in_=out_tiles[n][:])
 
+        def value_quarters(t):
+            if t < -1:
+                return []
+            if t < 3:
+                return [2 * (t + 1), 2 * (t + 1) + 1]
+            return [t + 5] if t + 5 < UNITS else []
+
         def step(t):
             if live(t - WEIGHT_LAG) and (t - WEIGHT_LAG) % 2 == 1:
                 weight_group_2((t - WEIGHT_LAG) // 2)
-            if live(t + VALUES_AHEAD):
-                regroup_values(t + VALUES_AHEAD)
+            for n in value_quarters(t):
+                regroup_values(n)
             if live(t - GROUP_2_LAG):
                 product(t - GROUP_2_LAG, 0)
             if live(t - GROUP_1_LAG):
@@ -407,8 +417,9 @@ def tile_mixerdiffattention_pb_t_kernel(
                 numerators(GROUPS * t)
             if live(t - GROUP_1_LAG):
                 add_group_1_and_store(t - GROUP_1_LAG)
-            if live(t - MOVE_LAG) and (t - MOVE_LAG) % Q_TILES == 0:
-                move_values((t - MOVE_LAG) // Q_TILES)
+            for n in value_quarters(t - 1):
+                if n % Q_TILES == Q_TILES - 1:
+                    move_values(n // Q_TILES)
             if live(t) and LOADS_AT_ONCE + t < len(later_loads):
                 load(LOADS_AT_ONCE + t)
             if live(t + INPUTS_AHEAD):
@@ -426,8 +437,10 @@ def tile_mixerdiffattention_pb_t_kernel(
                 quantise_e(b, (KEYS_OF_3, KEYS_OF_1, KEYS_OF_20)[turn])
             if live(t - INVERT_LAG) and (t - INVERT_LAG) % 2 == 1:
                 invert_row_sums((t - INVERT_LAG) // 2)
-            if live(t + VALUES_AHEAD):
-                quantise_values(t + VALUES_AHEAD)
+            for n in value_quarters(t):
+                quantise_values(n)
+            if t in (-4, -3):
+                clear_parts(t + 5)
 
         nc.vector.tensor_copy(out=mask_bf16[:], in_=mask_f32[:])
         for t in range(-INPUTS_AHEAD, 0):

@@ -38,14 +38,13 @@ WORDS = T // PACK
 SCALE_WORDS = F // PACK
 V_WORDS = F + SCALE_WORDS
 
-INPUTS_AHEAD = Q_TILES
-VALUE_BUFFERS = 4
-PART_BUFFERS = 3
+VALUE_BUFFERS = 3
+PART_BUFFERS = 2
 INVERT_LAG = 1
 WEIGHT_LAG = 2
 GROUP_2_LAG = 6
 GROUP_1_LAG = 7
-LOADS_AT_ONCE = 7
+LOADS_AT_ONCE = 6
 
 FLOPS = B * GROUPS * (2 * T * T * HD + 2 * T * T * F)
 
@@ -60,7 +59,7 @@ def tile_mixerdiffattention_pb_t_kernel(
         const = ctx.enter_context(tc.tile_pool(name="const", bufs=1))
         loads = ctx.enter_context(tc.tile_pool(name="loads", bufs=B))
         turned_inputs = ctx.enter_context(tc.tile_pool(name="turned_inputs", bufs=2 * GROUPS))
-        regrouped = ctx.enter_context(tc.tile_pool(name="regrouped", bufs=2))
+        regrouped = ctx.enter_context(tc.tile_pool(name="regrouped", bufs=4))
         stacks = ctx.enter_context(tc.tile_pool(name="stacks", bufs=2))
         grouped = ctx.enter_context(tc.tile_pool(name="grouped", bufs=2))
         quantised = ctx.enter_context(tc.tile_pool(name="quantised", bufs=2))
@@ -106,9 +105,10 @@ def tile_mixerdiffattention_pb_t_kernel(
 
         def clear_parts(n):
             for tiles in v_part.values():
-                nc.vector.memset(tiles[n][:].bitcast(I32), 0)
+                nc.gpsimd.memset(tiles[n][:].bitcast(F32), 0.0)
 
-        clear_parts(0)
+        for n in range(PART_BUFFERS):
+            clear_parts(n)
 
         q_heads, k_heads, v_in = [], [], []
         lam_in = const.tile([P, 4, LAM_LEN], BF16)
@@ -141,7 +141,7 @@ def tile_mixerdiffattention_pb_t_kernel(
         later_loads = []
         for b in range(1, B):
             later_loads += [("k", b), ("q", b), ("v", b)]
-        later_loads = [("k", 1), ("v", 0), ("q", 1), ("v", 1)] + later_loads[3:]
+        later_loads = [("k", 1), ("v", 0), ("q", 1), ("k", 2), ("v", 1), ("q", 2)] + later_loads[5:]
 
         def load(n):
             letter, b = later_loads[n]
@@ -394,16 +394,19 @@ def tile_mixerdiffattention_pb_t_kernel(
             nc.sync.dma_start(out=out[b, i * P : (i + 1) * P, :], in_=out_tiles[n][:])
 
         def value_quarters(t):
-            if t < -1:
+            if t < 2:
                 return []
-            if t < 3:
-                return [2 * (t + 1), 2 * (t + 1) + 1]
-            return [t + 5] if t + 5 < UNITS else []
+            if t < 6:
+                return [2 * t - 4, 2 * t - 3]
+            return [t + 2] if t + 2 < UNITS else []
+
+        def input_quarters(t):
+            return {-2: [0], -1: [1], 0: [2, 3, 4]}.get(t, [t + Q_TILES] if t + Q_TILES < UNITS else [])
 
         def step(t):
             if live(t - WEIGHT_LAG) and (t - WEIGHT_LAG) % 2 == 1:
                 weight_group_2((t - WEIGHT_LAG) // 2)
-            for n in value_quarters(t):
+            for n in value_quarters(t + 1):
                 regroup_values(n)
             if live(t - GROUP_2_LAG):
                 product(t - GROUP_2_LAG, 0)
@@ -422,8 +425,8 @@ def tile_mixerdiffattention_pb_t_kernel(
                     move_values(n // Q_TILES)
             if live(t) and LOADS_AT_ONCE + t < len(later_loads):
                 load(LOADS_AT_ONCE + t)
-            if live(t + INPUTS_AHEAD):
-                turn_input(t + INPUTS_AHEAD)
+            for n in input_quarters(t):
+                turn_input(n)
             if live(t - 2):
                 b, turn = divmod(t - 2, Q_TILES)
                 turn_e(b, *((KEYS_OF_3, 0, 1), (KEYS_OF_3, 1, 1), (KEYS_OF_1, 0, 1), (KEYS_OF_20, 0, 2))[turn])
@@ -439,14 +442,11 @@ def tile_mixerdiffattention_pb_t_kernel(
                 invert_row_sums((t - INVERT_LAG) // 2)
             for n in value_quarters(t):
                 quantise_values(n)
-            if t in (-4, -3):
-                clear_parts(t + 5)
 
         nc.vector.tensor_copy(out=mask_bf16[:], in_=mask_f32[:])
-        for t in range(-INPUTS_AHEAD, 0):
-            step(t)
-        compute_neg_lam()
-        for t in range(0, UNITS + GROUP_1_LAG):
+        for t in range(-2, UNITS + GROUP_1_LAG):
+            if t == 1:
+                compute_neg_lam()
             if t == WEIGHT_LAG:
                 spread_neg_lam()
             step(t)

@@ -34,6 +34,8 @@ HEAD_AT_PLACE = (1, 0)
 TILE_ORDER = (0, 3, 1, 2)
 PRODUCT_ORDER = (3, 1, 2, 0)
 KEYS_OF_3, KEYS_OF_20, KEYS_OF_1 = "tile 3", "tiles 2 and 0", "tile 1"
+STACK_OF_TILE = {3: KEYS_OF_3, 2: KEYS_OF_20, 0: KEYS_OF_20, 1: KEYS_OF_1}
+VALUES_LAG = 1
 WORDS = T // PACK
 SCALE_WORDS = F // PACK
 V_WORDS = F + SCALE_WORDS
@@ -59,10 +61,10 @@ def tile_mixerdiffattention_pb_t_kernel(
         const = ctx.enter_context(tc.tile_pool(name="const", bufs=1))
         loads = ctx.enter_context(tc.tile_pool(name="loads", bufs=B))
         turned_inputs = ctx.enter_context(tc.tile_pool(name="turned_inputs", bufs=2 * GROUPS))
-        regrouped = ctx.enter_context(tc.tile_pool(name="regrouped", bufs=4))
+        regrouped = ctx.enter_context(tc.tile_pool(name="regrouped", bufs=1))
         stacks = ctx.enter_context(tc.tile_pool(name="stacks", bufs=2))
-        grouped = ctx.enter_context(tc.tile_pool(name="grouped", bufs=2))
-        quantised = ctx.enter_context(tc.tile_pool(name="quantised", bufs=2))
+        grouped = ctx.enter_context(tc.tile_pool(name="grouped", bufs=3))
+        quantised = ctx.enter_context(tc.tile_pool(name="quantised", bufs=6))
         stats = ctx.enter_context(tc.tile_pool(name="stats", bufs=GROUP_1_LAG + 2))
         pair_stats = ctx.enter_context(tc.tile_pool(name="pair_stats", bufs=8))
         results = ctx.enter_context(tc.tile_pool(name="results", bufs=8))
@@ -98,8 +100,13 @@ def tile_mixerdiffattention_pb_t_kernel(
 
         v_whole = value_tiles("v_whole", VALUE_BUFFERS)
         v_part = {}
-        for key in ((2, 0), (0, 0), (1, 0), (1, 1)):
-            v_part[key] = value_tiles("v_part_%d_%d" % key, PART_BUFFERS)
+        for i in (2, 0):
+            v_part[i] = value_tiles("v_part_%d" % i, PART_BUFFERS)
+        e_of_1 = []
+        for n in range(2):
+            e_tile = const.tile([P, GROUPS, PLANES, T // PLANES], BF16, name="e_of_1_%d" % n)
+            nc.gpsimd.memset(e_tile[:].rearrange("p n a c -> p (n a c)").bitcast(F32), 0.0)
+            e_of_1.append(e_tile)
         for v_tile in v_whole:
             nc.vector.memset(v_tile[:, F:].bitcast(I32), 0)
 
@@ -241,14 +248,13 @@ def tile_mixerdiffattention_pb_t_kernel(
             )
 
         def move_values(b):
-            whole = v_whole[b % len(v_whole)]
-            for (i, place), tiles in v_part.items():
-                rows = (i + 1) * P // PACK
-                first = {2: 0, 0: WORDS - rows, 1: place * rows}[i]
-                nc.sync.dma_start(
-                    out=tiles[b % len(tiles)][first : first + rows, :].bitcast(I32),
-                    in_=whole[0:rows, :].bitcast(I32),
-                )
+            whole = v_whole[b % VALUE_BUFFERS]
+            rows = 3 * P // PACK
+            nc.gpsimd.tensor_copy(out=v_part[2][b % PART_BUFFERS][0:rows, :], in_=whole[0:rows, :])
+            nc.sync.dma_start(
+                out=v_part[0][b % PART_BUFFERS][rows:, :].bitcast(I32),
+                in_=whole[0 : P // PACK, :].bitcast(I32),
+            )
 
         def scores(h):
             u, place = half_unit(h)
@@ -284,14 +290,15 @@ def tile_mixerdiffattention_pb_t_kernel(
             if member == 0 and place == 0:
                 sums = pair_stats.tile([P, 2, GROUPS], F32)
                 row_sum[pair] = sums
-            stack = {3: KEYS_OF_3, 2: KEYS_OF_20, 0: KEYS_OF_20, 1: KEYS_OF_1}[i]
-            if (b, stack) not in e_stack:
-                width = 1 if stack == KEYS_OF_1 else GROUPS
-                e_tile = stacks.tile([P, width, PLANES, T // PLANES], BF16, name="e_" + stack.replace(" ", "_"))
+            stack = STACK_OF_TILE[i]
+            if stack == KEYS_OF_1:
+                e_stack[b, stack] = e_of_1[b % len(e_of_1)]
+            elif (b, stack) not in e_stack:
+                e_tile = stacks.tile([P, GROUPS, PLANES, T // PLANES], BF16, tag="e_" + stack)
                 e_stack[b, stack] = e_tile
             half = n_keys // PLANES
-            first = {3: 0, 2: 0, 0: T // PLANES - half, 1: place * half}[i]
-            e_out = e_stack[b, stack][:, 0 if i == 1 else place, :, first : first + half]
+            first = T // PLANES - half if i == 0 else 0
+            e_out = e_stack[b, stack][:, place, :, first : first + half]
             nc.scalar.activation(
                 out=e_out.rearrange("p a (w c) -> p a w c", c=2),
                 in_=s_banks[h][:, :n_keys].rearrange("p (w a c) -> p a w c", a=PLANES, c=2),
@@ -315,33 +322,25 @@ def tile_mixerdiffattention_pb_t_kernel(
                 op1=ALU.add,
             )
 
-        def turn_e(b, stack, first, count):
+        def turn_e(b, stack):
             e_words = e_stack[b, stack][:].bitcast(F32)
-            width = e_words.shape[1]
             bank = psum.tile([P, T], F32, tag="bank")
-            for n in range(count):
+            for place in range(GROUPS):
                 for plane in range(PLANES):
-                    column = (PLANES * n + plane) * P
+                    column = (PLANES * place + plane) * P
                     nc.tensor.transpose(
-                        bank[:, column : column + P], e_words[:, first + n, plane, :], ident_f32[:]
+                        bank[:, column : column + P], e_words[:, place, plane, :], ident_f32[:]
                     )
-            if first == 0:
-                keys_together = grouped.tile(
-                    [P, width * P, PACK], BF16, align_bytes=64, name="grouped_" + stack.replace(" ", "_")
-                )
-                e_grouped[b, stack] = keys_together
+            keys_together = grouped.tile([P, GROUPS * P, PACK], BF16, align_bytes=64)
             nc.scalar.copy(
-                out=e_grouped[b, stack][:]
-                .bitcast(F32)[:, first * P : (first + count) * P, :]
-                .rearrange("p (n r) a -> p n r a", n=count),
-                in_=bank[:, : count * PLANES * P].rearrange("p (n a r) -> p n r a", n=count, a=PLANES),
+                out=keys_together[:].bitcast(F32).rearrange("p (n r) a -> p n r a", n=GROUPS),
+                in_=bank[:].rearrange("p (n a r) -> p n r a", n=GROUPS, a=PLANES),
             )
+            e_grouped[b, stack] = keys_together
 
         def quantise_e(b, stack):
-            name = stack.replace(" ", "_")
-            columns = e_grouped[b, stack].shape[1]
-            codes = quantised.tile([P, columns], U32, align_bytes=64, name="codes_" + name)
-            scales = quantised.tile([P, columns], U8, align_bytes=64, name="scales_" + name)
+            codes = quantised.tile([P, GROUPS * P], U32, align_bytes=64)
+            scales = quantised.tile([P, GROUPS * P], U8, align_bytes=64)
             nc.vector.quantize_mx(
                 out=codes[:].bitcast(FP8X4),
                 scales=scales[:],
@@ -356,10 +355,9 @@ def tile_mixerdiffattention_pb_t_kernel(
 
         def product(n, place):
             b, i, pair, member = product_unit(n)
-            stack = {3: KEYS_OF_3, 2: KEYS_OF_20, 0: KEYS_OF_20, 1: KEYS_OF_1}[i]
-            column = 0 if i == 1 else place * P
-            queries = slice(column, column + P)
-            v_tiles = v_whole if i == 3 else v_part[i, place if i == 1 else 0]
+            stack = STACK_OF_TILE[i]
+            queries = slice(place * P, (place + 1) * P)
+            v_tiles = v_part.get(i, v_whole)
             v_tile = v_tiles[b % len(v_tiles)]
             bank = psum.tile([P, F], F32, tag="bank")
             nc.tensor.matmul_mx(
@@ -393,21 +391,16 @@ def tile_mixerdiffattention_pb_t_kernel(
             )
             nc.sync.dma_start(out=out[b, i * P : (i + 1) * P, :], in_=out_tiles[n][:])
 
-        def value_quarters(t):
-            if t < 2:
-                return []
-            if t < 6:
-                return [2 * t - 4, 2 * t - 3]
-            return [t + 2] if t + 2 < UNITS else []
-
         def input_quarters(t):
             return {-2: [0], -1: [1], 0: [2, 3, 4]}.get(t, [t + Q_TILES] if t + Q_TILES < UNITS else [])
 
         def step(t):
             if live(t - WEIGHT_LAG) and (t - WEIGHT_LAG) % 2 == 1:
                 weight_group_2((t - WEIGHT_LAG) // 2)
-            for n in value_quarters(t + 1):
-                regroup_values(n)
+            if live(t - VALUES_LAG):
+                regroup_values(t - VALUES_LAG)
+            if live(t - VALUES_LAG - 4) and (t - VALUES_LAG) % Q_TILES == 0:
+                move_values((t - VALUES_LAG) // Q_TILES - 1)
             if live(t - GROUP_2_LAG):
                 product(t - GROUP_2_LAG, 0)
             if live(t - GROUP_1_LAG):
@@ -420,16 +413,13 @@ def tile_mixerdiffattention_pb_t_kernel(
                 numerators(GROUPS * t)
             if live(t - GROUP_1_LAG):
                 add_group_1_and_store(t - GROUP_1_LAG)
-            for n in value_quarters(t - 1):
-                if n % Q_TILES == Q_TILES - 1:
-                    move_values(n // Q_TILES)
             if live(t) and LOADS_AT_ONCE + t < len(later_loads):
                 load(LOADS_AT_ONCE + t)
             for n in input_quarters(t):
                 turn_input(n)
-            if live(t - 2):
-                b, turn = divmod(t - 2, Q_TILES)
-                turn_e(b, *((KEYS_OF_3, 0, 1), (KEYS_OF_3, 1, 1), (KEYS_OF_1, 0, 1), (KEYS_OF_20, 0, 2))[turn])
+            if live(t - 3) and (t - 3) % Q_TILES < 3:
+                b, turn = divmod(t - 3, Q_TILES)
+                turn_e(b, (KEYS_OF_3, KEYS_OF_1, KEYS_OF_20)[turn])
             if live(t + 1):
                 scores(GROUPS * (t + 1))
                 row_maximum(GROUPS * (t + 1))
@@ -440,8 +430,8 @@ def tile_mixerdiffattention_pb_t_kernel(
                 quantise_e(b, (KEYS_OF_3, KEYS_OF_1, KEYS_OF_20)[turn])
             if live(t - INVERT_LAG) and (t - INVERT_LAG) % 2 == 1:
                 invert_row_sums((t - INVERT_LAG) // 2)
-            for n in value_quarters(t):
-                quantise_values(n)
+            if live(t - VALUES_LAG):
+                quantise_values(t - VALUES_LAG)
 
         nc.vector.tensor_copy(out=mask_bf16[:], in_=mask_f32[:])
         for t in range(-2, UNITS + GROUP_1_LAG):

@@ -23,32 +23,31 @@ HD = 256
 F = 512
 LAM_LEN = 128
 Q_TILES = T // P
-PAIRS = HD // 2
 PLANES = 2
+WORDS = T // PACK
 SCORE_SCALE = 1.0 / math.sqrt(HD)
 LAMBDA_INIT = 0.8 - 0.6 * math.exp(-0.3 * 0)
 MASKED = -1.0e30
-
-UNITS = B * Q_TILES
 HEAD_AT_PLACE = (1, 0)
-TILE_ORDER = (0, 3, 1, 2)
-PRODUCT_ORDER = (3, 1, 2, 0)
-KEYS_OF_3, KEYS_OF_20, KEYS_OF_1 = "tile 3", "tiles 2 and 0", "tile 1"
-STACK_OF_TILE = {3: KEYS_OF_3, 2: KEYS_OF_20, 0: KEYS_OF_20, 1: KEYS_OF_1}
-VALUES_LAG = 1
-WORDS = T // PACK
-SCALE_WORDS = F // PACK
-V_WORDS = F + SCALE_WORDS
-
-VALUE_BUFFERS = 3
-PART_BUFFERS = 2
-INVERT_LAG = 1
-WEIGHT_LAG = 2
-GROUP_2_LAG = 6
-GROUP_1_LAG = 7
-LOADS_AT_ONCE = 6
 
 FLOPS = B * GROUPS * (2 * T * T * HD + 2 * T * T * F)
+
+TILE_ORDER = (0, 3, 1, 2)
+PRODUCT_ORDER = (3, 1, 2, 0)
+STACK_OF_TILE = {3: "3", 2: "20", 0: "20", 1: "1"}
+HALVES = B * Q_TILES * GROUPS
+TURNS = HALVES // 2
+STACKS = ("3", "1", "20")
+E_LAG = 3
+QUANTISE_LAG = 4
+PRODUCT_LAG = 6
+SUMS_LAG = 4
+WEIGHT_LAG = 5
+VALUE_BUFFERS = 3
+MOVE_LAG = 3
+PART_BUFFERS = 2
+LOADS_AT_ONCE = 6
+LOAD_LEAD = 6
 
 
 def tile_mixerdiffattention_pb_t_kernel(
@@ -64,9 +63,9 @@ def tile_mixerdiffattention_pb_t_kernel(
         regrouped = ctx.enter_context(tc.tile_pool(name="regrouped", bufs=1))
         stacks = ctx.enter_context(tc.tile_pool(name="stacks", bufs=2))
         grouped = ctx.enter_context(tc.tile_pool(name="grouped", bufs=3))
-        quantised = ctx.enter_context(tc.tile_pool(name="quantised", bufs=6))
-        stats = ctx.enter_context(tc.tile_pool(name="stats", bufs=GROUP_1_LAG + 2))
-        pair_stats = ctx.enter_context(tc.tile_pool(name="pair_stats", bufs=8))
+        quantised = ctx.enter_context(tc.tile_pool(name="quantised", bufs=5))
+        stats = ctx.enter_context(tc.tile_pool(name="stats", bufs=8))
+        sums = ctx.enter_context(tc.tile_pool(name="sums", bufs=4))
         results = ctx.enter_context(tc.tile_pool(name="results", bufs=8))
         psum = ctx.enter_context(tc.psum_pool(name="psum", bufs=8))
 
@@ -91,31 +90,30 @@ def tile_mixerdiffattention_pb_t_kernel(
         one_column = const.tile([P, 1], F32)
         nc.scalar.activation(out=one_column[:], in_=zero_column[:], func=ACT.Exp)
 
-        def value_tiles(name, count):
+        def value_tiles(name, dtype, count):
             tiles = []
             for n in range(count):
-                v_tile = const.tile([P, V_WORDS], U32, name="%s_%d" % (name, n), align_bytes=64)
+                v_tile = const.tile([P, F], dtype, name="%s_%d" % (name, n), align_bytes=256)
                 tiles.append(v_tile)
             return tiles
 
-        v_whole = value_tiles("v_whole", VALUE_BUFFERS)
-        v_part = {}
+        v_codes = value_tiles("v_codes", U32, VALUE_BUFFERS)
+        v_scales = value_tiles("v_scales", U8, VALUE_BUFFERS)
+        part_codes = {}
         for i in (2, 0):
-            v_part[i] = value_tiles("v_part_%d" % i, PART_BUFFERS)
+            part_codes[i] = value_tiles("part_codes_%d" % i, U32, PART_BUFFERS)
+        part_scales = value_tiles("part_scales", U8, PART_BUFFERS)
+        for tile_list in (v_scales, part_scales):
+            for v_tile in tile_list:
+                nc.vector.memset(v_tile[:].bitcast(I32), 0)
+        for tile_list in part_codes.values():
+            for v_tile in tile_list:
+                nc.gpsimd.memset(v_tile[:].bitcast(F32), 0.0)
         e_of_1 = []
         for n in range(2):
             e_tile = const.tile([P, GROUPS, PLANES, T // PLANES], BF16, name="e_of_1_%d" % n)
-            nc.gpsimd.memset(e_tile[:].rearrange("p n a c -> p (n a c)").bitcast(F32), 0.0)
+            nc.vector.memset(e_tile[:], 0.0)
             e_of_1.append(e_tile)
-        for v_tile in v_whole:
-            nc.vector.memset(v_tile[:, F:].bitcast(I32), 0)
-
-        def clear_parts(n):
-            for tiles in v_part.values():
-                nc.gpsimd.memset(tiles[n][:].bitcast(F32), 0.0)
-
-        for n in range(PART_BUFFERS):
-            clear_parts(n)
 
         q_heads, k_heads, v_in = [], [], []
         lam_in = const.tile([P, 4, LAM_LEN], BF16)
@@ -147,8 +145,8 @@ def tile_mixerdiffattention_pb_t_kernel(
             nc.sync.dma_start(out=lam_in[0:1, n, :], in_=vec.rearrange("(o n) -> o n", o=1))
         later_loads = []
         for b in range(1, B):
-            later_loads += [("k", b), ("q", b), ("v", b)]
-        later_loads = [("k", 1), ("v", 0), ("q", 1), ("k", 2), ("v", 1), ("q", 2)] + later_loads[5:]
+            later_loads += [("k", b), ("v", b - 1), ("q", b)]
+        later_loads.append(("v", B - 1))
 
         def load(n):
             letter, b = later_loads[n]
@@ -192,41 +190,35 @@ def tile_mixerdiffattention_pb_t_kernel(
             nc.tensor.matmul(bank[:, 0:2], lhsT=first_row[:], rhs=lam_column[:], start=True, stop=True)
             nc.vector.tensor_copy(out=neg_lam[:], in_=bank[:, 0:1])
 
-        qT, kT = {}, {}
-        v_grouped = {}
-        e_stack = {}
-        s_banks, neg_max, row_sum, weight = {}, {}, {}, {}
-        e_grouped, e_codes, e_scales = {}, {}, {}
-        y_banks, out_tiles = {}, {}
+        qT, kT, v_grouped = {}, {}, {}
+        s_columns, neg_max, row_sum, weight = {}, {}, {}, {}
+        e_stack, e_bank, e_grouped, e_codes, e_scales = {}, {}, {}, {}, {}
+        kq_bank, y_bank, result_of = {}, {}, {}
 
-        def live(u):
-            return 0 <= u < UNITS
-
-        def half_unit(h):
-            turn, second = divmod(h, 2)
-            two_units, place = divmod(turn, GROUPS)
-            return 2 * two_units + second, place
-
-        def turn_input(u):
-            b, quarter = divmod(u, Q_TILES)
+        def turn_input(b, quarter):
             place = quarter // 2
-            source, turned = ((k_heads, kT), (q_heads, qT))[quarter % 2]
+            source = (k_heads, q_heads)[quarter % 2]
             words = source[b][HEAD_AT_PLACE[place]].bitcast(F32)
             bank = psum.tile([P, T], F32, tag="bank")
             for j in range(Q_TILES):
                 nc.tensor.transpose(bank[:, j * P : (j + 1) * P], words[:, j, :], ident_f32[:])
+            kq_bank[b, quarter] = bank
+
+        def take_input(b, quarter):
+            bank = kq_bank[b, quarter]
             rows = turned_inputs.tile([P, T, 2], BF16, tag="turned%d" % (quarter % 2))
             if quarter % 2 == 0:
                 nc.scalar.copy(out=rows[:].bitcast(F32).rearrange("p r w -> p (r w)"), in_=bank[:])
+                kT[b, quarter // 2] = rows
             else:
                 nc.vector.tensor_scalar_mul(
                     out=rows[:].rearrange("p r w -> p (r w)"), in0=bank[:].bitcast(BF16), scalar1=SCORE_SCALE
                 )
-            turned[b, place] = rows
+                qT[b, quarter // 2] = rows
 
-        def regroup_values(u):
-            b, quarter = divmod(u, Q_TILES)
-            keys_together = regrouped.tile([P, P, PACK], BF16, align_bytes=64)
+        def regroup_values(n, slot):
+            b, quarter = divmod(n, 4)
+            keys_together = regrouped.tile([P, P, PACK], BF16, align_bytes=64, tag="regrouped%d" % slot)
             nc.gpsimd.tensor_scalar(
                 out=keys_together[:],
                 in0=v_in[b][:, :, quarter * P : (quarter + 1) * P].rearrange("p t f -> p f t"),
@@ -235,87 +227,90 @@ def tile_mixerdiffattention_pb_t_kernel(
                 op0=ALU.mult,
                 op1=ALU.add,
             )
-            v_grouped[u] = keys_together
+            v_grouped[n] = keys_together
 
-        def quantise_values(u):
-            b, quarter = divmod(u, Q_TILES)
+        def quantise_values(n):
+            b, quarter = divmod(n, 4)
             features = slice(quarter * P, (quarter + 1) * P)
-            v_tile = v_whole[b % len(v_whole)]
             nc.vector.quantize_mx(
-                out=v_tile[:, features].bitcast(FP8X4),
-                scales=v_tile[:, F:].bitcast(U8)[:, features],
-                in_=v_grouped[u][:].rearrange("p f t -> p (f t)"),
+                out=v_codes[b % VALUE_BUFFERS][:, features].bitcast(FP8X4),
+                scales=v_scales[b % VALUE_BUFFERS][:, features],
+                in_=v_grouped[n][:].rearrange("p f t -> p (f t)"),
             )
 
         def move_values(b):
-            whole = v_whole[b % VALUE_BUFFERS]
+            rows = P // PACK
+            for to, source in (
+                (part_codes[0][b % PART_BUFFERS], v_codes[b % VALUE_BUFFERS]),
+                (part_scales[b % PART_BUFFERS], v_scales[b % VALUE_BUFFERS]),
+            ):
+                nc.sync.dma_start(out=to[WORDS - rows :, :].bitcast(I32), in_=source[:rows, :].bitcast(I32))
+
+        def copy_values(b):
             rows = 3 * P // PACK
-            nc.gpsimd.tensor_copy(out=v_part[2][b % PART_BUFFERS][0:rows, :], in_=whole[0:rows, :])
-            nc.sync.dma_start(
-                out=v_part[0][b % PART_BUFFERS][rows:, :].bitcast(I32),
-                in_=whole[0 : P // PACK, :].bitcast(I32),
+            nc.gpsimd.tensor_copy(
+                out=part_codes[2][b % PART_BUFFERS][:rows, :], in_=v_codes[b % VALUE_BUFFERS][:rows, :]
             )
 
+        def half(h):
+            turn, second = divmod(h, 2)
+            two_tiles, place = divmod(turn, GROUPS)
+            b, n = divmod(2 * two_tiles + second, Q_TILES)
+            return b, TILE_ORDER[n], place
+
         def scores(h):
-            u, place = half_unit(h)
-            b, i = u // Q_TILES, TILE_ORDER[u % Q_TILES]
+            b, i, place = half(h)
             rows = slice(i * P, (i + 1) * P)
             n_keys = (i + 1) * P
             queries, keys = qT[b, place], kT[b, place]
             bank = psum.tile([P, T], F32, tag="bank")
-            nc.tensor.matmul(
-                bank[:, :n_keys], lhsT=queries[:, rows, 0], rhs=keys[:, :n_keys, 0], start=True, stop=False
-            )
+            s = bank[:, :n_keys]
+            nc.tensor.matmul(s, lhsT=queries[:, rows, 0], rhs=keys[:, :n_keys, 0], start=True, stop=False)
             nc.tensor.matmul(bank[:, rows], lhsT=ident_bf16[:], rhs=mask_bf16[:], start=False, stop=False)
-            nc.tensor.matmul(
-                bank[:, :n_keys], lhsT=queries[:, rows, 1], rhs=keys[:, :n_keys, 1], start=False, stop=True
-            )
-            s_banks[h] = bank
+            nc.tensor.matmul(s, lhsT=queries[:, rows, 1], rhs=keys[:, :n_keys, 1], start=False, stop=True)
+            s_columns[h] = s
 
         def row_maximum(h):
-            u, place = half_unit(h)
-            n_keys = (TILE_ORDER[u % Q_TILES] + 1) * P
+            b, i, place = half(h)
             if place == 0:
-                maxima = stats.tile([P, GROUPS], F32)
-                neg_max[u] = maxima
+                maxima = stats.tile([P, GROUPS], F32, tag="neg_max")
+                neg_max[b, i] = maxima
             nc.vector.reduce_max(
-                out=neg_max[u][:, place : place + 1], in_=s_banks[h][:, :n_keys], axis=AX.X, negate=True
+                out=neg_max[b, i][:, place : place + 1], in_=s_columns[h], axis=AX.X, negate=True
             )
 
         def numerators(h):
-            u, place = half_unit(h)
-            b, i = u // Q_TILES, TILE_ORDER[u % Q_TILES]
+            b, i, place = half(h)
             n_keys = (i + 1) * P
-            pair, member = divmod(u, 2)
-            if member == 0 and place == 0:
-                sums = pair_stats.tile([P, 2, GROUPS], F32)
-                row_sum[pair] = sums
+            if b not in row_sum:
+                row_sums = sums.tile([P, Q_TILES, GROUPS], F32, tag="row_sum")
+                row_sum[b] = row_sums
             stack = STACK_OF_TILE[i]
-            if stack == KEYS_OF_1:
+            if i == 1:
                 e_stack[b, stack] = e_of_1[b % len(e_of_1)]
             elif (b, stack) not in e_stack:
                 e_tile = stacks.tile([P, GROUPS, PLANES, T // PLANES], BF16, tag="e_" + stack)
                 e_stack[b, stack] = e_tile
-            half = n_keys // PLANES
-            first = T // PLANES - half if i == 0 else 0
-            e_out = e_stack[b, stack][:, place, :, first : first + half]
+            width = n_keys // PLANES
+            first = T // PLANES - width if i == 0 else 0
+            e_out = e_stack[b, stack][:, place, :, first : first + width]
             nc.scalar.activation(
                 out=e_out.rearrange("p a (w c) -> p a w c", c=2),
-                in_=s_banks[h][:, :n_keys].rearrange("p (w a c) -> p a w c", a=PLANES, c=2),
+                in_=s_columns[h].rearrange("p (w a c) -> p a w c", a=PLANES, c=2),
                 func=ACT.Exp,
-                bias=neg_max[u][:, place : place + 1],
-                accum_out=row_sum[pair][:, member, place : place + 1],
+                bias=neg_max[b, i][:, place : place + 1],
+                accum_out=row_sum[b][:, i, place : place + 1],
             )
 
-        def invert_row_sums(pair):
-            factors = pair_stats.tile([P, 2, GROUPS], F32)
-            nc.vector.reciprocal(out=factors[:], in_=row_sum[pair][:])
-            weight[pair] = factors
+        def invert_row_sums(b):
+            factors = sums.tile([P, Q_TILES, GROUPS], F32, tag="weight")
+            nc.vector.reciprocal(out=factors[:], in_=row_sum[b][:])
+            weight[b] = factors
 
-        def weight_group_2(pair):
+        def weight_group_2(b):
             nc.gpsimd.tensor_scalar(
-                out=weight[pair][:, :, 0],
-                in0=weight[pair][:, :, 0],
+                out=weight[b][:, :, 0],
+                in0=weight[b][:, :, 0],
                 scalar1=neg_lam[:, 0:1],
                 scalar2=0.0,
                 op0=ALU.mult,
@@ -328,19 +323,20 @@ def tile_mixerdiffattention_pb_t_kernel(
             for place in range(GROUPS):
                 for plane in range(PLANES):
                     column = (PLANES * place + plane) * P
-                    nc.tensor.transpose(
-                        bank[:, column : column + P], e_words[:, place, plane, :], ident_f32[:]
-                    )
-            keys_together = grouped.tile([P, GROUPS * P, PACK], BF16, align_bytes=64)
+                    nc.tensor.transpose(bank[:, column : column + P], e_words[:, place, plane, :], ident_f32[:])
+            e_bank[b, stack] = bank
+
+        def take_e(b, stack):
+            keys_together = grouped.tile([P, GROUPS * P, PACK], BF16, align_bytes=64, tag="grouped")
             nc.scalar.copy(
                 out=keys_together[:].bitcast(F32).rearrange("p (n r) a -> p n r a", n=GROUPS),
-                in_=bank[:].rearrange("p (n a r) -> p n r a", n=GROUPS, a=PLANES),
+                in_=e_bank[b, stack][:].rearrange("p (n a r) -> p n r a", n=GROUPS, a=PLANES),
             )
             e_grouped[b, stack] = keys_together
 
         def quantise_e(b, stack):
-            codes = quantised.tile([P, GROUPS * P], U32, align_bytes=64)
-            scales = quantised.tile([P, GROUPS * P], U8, align_bytes=64)
+            codes = quantised.tile([P, GROUPS * P], U32, align_bytes=64, tag="codes")
+            scales = quantised.tile([P, GROUPS * P], U8, align_bytes=64, tag="scales")
             nc.vector.quantize_mx(
                 out=codes[:].bitcast(FP8X4),
                 scales=scales[:],
@@ -348,95 +344,130 @@ def tile_mixerdiffattention_pb_t_kernel(
             )
             e_codes[b, stack], e_scales[b, stack] = codes, scales
 
-        def product_unit(n):
-            b, i = n // Q_TILES, PRODUCT_ORDER[n % Q_TILES]
-            pair, member = divmod(b * Q_TILES + TILE_ORDER.index(i), 2)
-            return b, i, pair, member
-
         def product(n, place):
-            b, i, pair, member = product_unit(n)
+            b, i = n // Q_TILES, PRODUCT_ORDER[n % Q_TILES]
             stack = STACK_OF_TILE[i]
             queries = slice(place * P, (place + 1) * P)
-            v_tiles = v_part.get(i, v_whole)
-            v_tile = v_tiles[b % len(v_tiles)]
+            codes, scales = v_codes[b % VALUE_BUFFERS], v_scales[b % VALUE_BUFFERS]
+            if i in part_codes:
+                codes = part_codes[i][b % PART_BUFFERS]
+            if i == 0:
+                scales = part_scales[b % PART_BUFFERS]
             bank = psum.tile([P, F], F32, tag="bank")
             nc.tensor.matmul_mx(
                 out=bank[:],
                 lhsT=e_codes[b, stack][:, queries].bitcast(FP8X4),
                 lhsT_scale=e_scales[b, stack][:, queries],
-                rhs=v_tile[:, :F].bitcast(FP8X4),
-                rhs_scale=v_tile[:, F:].bitcast(U8),
+                rhs=codes[:].bitcast(FP8X4),
+                rhs_scale=scales[:],
                 start=True,
                 stop=True,
             )
-            y_banks[GROUPS * n + place] = bank
+            y_bank[b, i, place] = bank
 
-        def weigh_group_2(n):
-            b, i, pair, member = product_unit(n)
-            result = results.tile([P, F], F32)
-            nc.scalar.activation(
-                out=result[:], in_=y_banks[GROUPS * n][:], func=ACT.Copy, scale=weight[pair][:, member, 0:1]
-            )
-            out_tiles[n] = result
+        def take_product(n, place):
+            b, i = n // Q_TILES, PRODUCT_ORDER[n % Q_TILES]
+            if place == 0:
+                result = results.tile([P, F], F32, tag="result")
+                nc.scalar.activation(
+                    out=result[:], in_=y_bank[b, i, 0][:], func=ACT.Copy, scale=weight[b][:, i, 0:1]
+                )
+                result_of[b, i] = result
+            else:
+                nc.vector.scalar_tensor_tensor(
+                    out=result_of[b, i][:],
+                    in0=y_bank[b, i, 1][:],
+                    scalar=weight[b][:, i, 1:2],
+                    in1=result_of[b, i][:],
+                    op0=ALU.mult,
+                    op1=ALU.add,
+                )
+                nc.sync.dma_start(out=out[b, i * P : (i + 1) * P, :], in_=result_of[b, i][:])
 
-        def add_group_1_and_store(n):
-            b, i, pair, member = product_unit(n)
-            nc.vector.scalar_tensor_tensor(
-                out=out_tiles[n][:],
-                in0=y_banks[GROUPS * n + 1][:],
-                scalar=weight[pair][:, member, 1:2],
-                in1=out_tiles[n][:],
-                op0=ALU.mult,
-                op1=ALU.add,
-            )
-            nc.sync.dma_start(out=out[b, i * P : (i + 1) * P, :], in_=out_tiles[n][:])
 
         def input_quarters(t):
-            return {-2: [0], -1: [1], 0: [2, 3, 4]}.get(t, [t + Q_TILES] if t + Q_TILES < UNITS else [])
+            if t < 0:
+                return {-2: (0, 1), -1: (2, 3)}[t]
+            return (t + Q_TILES,) if t + Q_TILES < 4 * B else ()
+
+        def value_quarters(t):
+            if t < 1:
+                return []
+            if t < 3:
+                return [2 * t - 2, 2 * t - 1]
+            return [t + 1] if t + 1 < 4 * B else []
+
+        def loads_of_turn(t):
+            entry, turn = divmod(t + LOAD_LEAD, Q_TILES)
+            n = 3 * entry + turn
+            if turn < 3 and LOADS_AT_ONCE <= n < len(later_loads):
+                return [n]
+            return []
 
         def step(t):
-            if live(t - WEIGHT_LAG) and (t - WEIGHT_LAG) % 2 == 1:
-                weight_group_2((t - WEIGHT_LAG) // 2)
-            if live(t - VALUES_LAG):
-                regroup_values(t - VALUES_LAG)
-            if live(t - VALUES_LAG - 4) and (t - VALUES_LAG) % Q_TILES == 0:
-                move_values((t - VALUES_LAG) // Q_TILES - 1)
-            if live(t - GROUP_2_LAG):
-                product(t - GROUP_2_LAG, 0)
-            if live(t - GROUP_1_LAG):
-                product(t - GROUP_1_LAG, 1)
-            if live(t - GROUP_2_LAG):
-                weigh_group_2(t - GROUP_2_LAG)
-            if live(t):
-                scores(GROUPS * t + 1)
-                row_maximum(GROUPS * t + 1)
-                numerators(GROUPS * t)
-            if live(t - GROUP_1_LAG):
-                add_group_1_and_store(t - GROUP_1_LAG)
-            if live(t) and LOADS_AT_ONCE + t < len(later_loads):
-                load(LOADS_AT_ONCE + t)
+            n_2, n_1 = t - PRODUCT_LAG, t - PRODUCT_LAG - 1
+            quarters = value_quarters(t)
+            b_e, e_turn = divmod(t - E_LAG, Q_TILES)
+            b_q, q_turn = divmod(t - QUANTISE_LAG, Q_TILES)
+            live_e = 0 <= b_e < B and e_turn < len(STACKS)
+            live_q = 0 <= b_q < B and q_turn < len(STACKS)
+
+            if 0 <= n_2 < TURNS:
+                product(n_2, 0)
+            if 0 <= n_1 < TURNS:
+                product(n_1, 1)
+            if 0 <= t < TURNS:
+                scores(2 * t + 1)
             for n in input_quarters(t):
-                turn_input(n)
-            if live(t - 3) and (t - 3) % Q_TILES < 3:
-                b, turn = divmod(t - 3, Q_TILES)
-                turn_e(b, (KEYS_OF_3, KEYS_OF_1, KEYS_OF_20)[turn])
-            if live(t + 1):
-                scores(GROUPS * (t + 1))
-                row_maximum(GROUPS * (t + 1))
-            if live(t):
-                numerators(GROUPS * t + 1)
-            if live(t - 4) and (t - 4) % Q_TILES < 3:
-                b, turn = divmod(t - 4, Q_TILES)
-                quantise_e(b, (KEYS_OF_3, KEYS_OF_1, KEYS_OF_20)[turn])
-            if live(t - INVERT_LAG) and (t - INVERT_LAG) % 2 == 1:
-                invert_row_sums((t - INVERT_LAG) // 2)
-            if live(t - VALUES_LAG):
-                quantise_values(t - VALUES_LAG)
+                turn_input(n // 4, n % 4)
+            if live_e:
+                turn_e(b_e, STACKS[e_turn])
+            if 0 <= t + 1 < TURNS:
+                scores(2 * t + 2)
+
+            if t % Q_TILES == WEIGHT_LAG % Q_TILES and 0 <= t - WEIGHT_LAG < TURNS:
+                weight_group_2((t - WEIGHT_LAG) // Q_TILES)
+            for slot, n in enumerate(quarters):
+                regroup_values(n, slot)
+            if t % Q_TILES == MOVE_LAG % Q_TILES and 0 <= t - MOVE_LAG < TURNS:
+                copy_values((t - MOVE_LAG) // Q_TILES)
+
+            if 0 <= t < TURNS:
+                row_maximum(2 * t + 1)
+            if 0 <= n_1 < TURNS:
+                take_product(n_1, 1)
+            if t % Q_TILES == MOVE_LAG % Q_TILES and 0 <= t - MOVE_LAG < TURNS:
+                move_values((t - MOVE_LAG) // Q_TILES)
+            for n in loads_of_turn(t):
+                load(n)
+            for n in input_quarters(t):
+                if n % 2 == 1:
+                    take_input(n // 4, n % 4)
+            if 0 <= t + 1 < TURNS:
+                row_maximum(2 * t + 2)
+            if live_q:
+                quantise_e(b_q, STACKS[q_turn])
+            if t % Q_TILES == SUMS_LAG % Q_TILES and 0 <= t - SUMS_LAG < TURNS:
+                invert_row_sums((t - SUMS_LAG) // Q_TILES)
+            for n in quarters:
+                quantise_values(n)
+
+            if 0 <= t < TURNS:
+                numerators(2 * t)
+            if 0 <= n_2 < TURNS:
+                take_product(n_2, 0)
+            for n in input_quarters(t):
+                if n % 2 == 0:
+                    take_input(n // 4, n % 4)
+            if 0 <= t < TURNS:
+                numerators(2 * t + 1)
+            if live_e:
+                take_e(b_e, STACKS[e_turn])
 
         nc.vector.tensor_copy(out=mask_bf16[:], in_=mask_f32[:])
-        for t in range(-2, UNITS + GROUP_1_LAG):
+        for t in range(-2, TURNS + PRODUCT_LAG + 1):
             if t == 1:
                 compute_neg_lam()
-            if t == WEIGHT_LAG:
+            if t == 2:
                 spread_neg_lam()
             step(t)

@@ -33,17 +33,17 @@ HEAD_AT_PLACE = (1, 0)
 FLOPS = B * GROUPS * (2 * T * T * HD + 2 * T * T * F)
 
 TILE_ORDER = (0, 3, 1, 2)
-PRODUCT_ORDER = (3, 1, 2, 0)
 STACK_OF_TILE = {3: "3", 2: "20", 0: "20", 1: "1"}
 HALVES = B * Q_TILES * GROUPS
 TURNS = HALVES // 2
-STACKS = ("3", "1", "20")
-E_LAG = 3
-QUANTISE_LAG = 4
-PRODUCT_LAG = 6
+PAIR = 2 * Q_TILES
+TRANSPOSES = ((3, 0, "3"), (5, 0, "20"), (7, 1, "3"), (8, 0, "1"), (9, 1, "20"))
+QUANTISE_LAG = 1
+PRODUCTS = ((0, 3), (0, 2), (0, 0), (1, 3), (0, 1), (1, 1), (1, 2), (1, 0))
+PRODUCT_LAG = 7
 SUMS_LAG = 4
 WEIGHT_LAG = 5
-VALUE_BUFFERS = 3
+VALUE_BUFFERS = 4
 MOVE_LAG = 3
 PART_BUFFERS = 2
 LOADS_AT_ONCE = 6
@@ -99,21 +99,23 @@ def tile_mixerdiffattention_pb_t_kernel(
 
         v_codes = value_tiles("v_codes", U32, VALUE_BUFFERS)
         v_scales = value_tiles("v_scales", U8, VALUE_BUFFERS)
-        part_codes = {}
-        for i in (2, 0):
-            part_codes[i] = value_tiles("part_codes_%d" % i, U32, PART_BUFFERS)
-        part_scales = value_tiles("part_scales", U8, PART_BUFFERS)
-        for tile_list in (v_scales, part_scales):
+        part_codes, part_scales = {}, {}
+        for name in ("2", "0", "1 first", "1 second"):
+            part_codes[name] = value_tiles("part_codes_" + name.replace(" ", "_"), U32, PART_BUFFERS)
+        for name in ("0", "1 second"):
+            part_scales[name] = value_tiles("part_scales_" + name.replace(" ", "_"), U8, PART_BUFFERS)
+        for tile_list in [v_scales] + list(part_scales.values()):
             for v_tile in tile_list:
                 nc.vector.memset(v_tile[:].bitcast(I32), 0)
-        for tile_list in part_codes.values():
+        for name, tile_list in part_codes.items():
+            engine = nc.vector if name in part_scales else nc.gpsimd
             for v_tile in tile_list:
-                nc.gpsimd.memset(v_tile[:].bitcast(F32), 0.0)
-        e_of_1 = []
-        for n in range(2):
-            e_tile = const.tile([P, GROUPS, PLANES, T // PLANES], BF16, name="e_of_1_%d" % n)
-            nc.vector.memset(e_tile[:], 0.0)
-            e_of_1.append(e_tile)
+                engine.memset(v_tile[:].bitcast(F32), 0.0)
+
+        def part_of(b, i):
+            if i == 1:
+                return ("1 first", "1 second")[b % 2], b // 2 % PART_BUFFERS
+            return str(i), b % PART_BUFFERS
 
         q_heads, k_heads, v_in = [], [], []
         lam_in = const.tile([P, 4, LAM_LEN], BF16)
@@ -167,15 +169,22 @@ def tile_mixerdiffattention_pb_t_kernel(
         nc.vector.memset(first_row[:], 0.0)
         nc.vector.memset(first_row[0:1, :], 1.0)
 
-        def compute_neg_lam():
-            products = const.tile([P, 2, LAM_LEN], F32)
+        lam_products = const.tile([P, 2, LAM_LEN], F32)
+        dots = const.tile([P, 2], F32)
+        exp_dots = const.tile([P, 2], F32)
+
+        def multiply_lambdas():
             nc.vector.tensor_tensor(
-                out=products[0:1], in0=lam_in[0:1, 0:2, :], in1=lam_in[0:1, 2:4, :], op=ALU.mult
+                out=lam_products[0:1], in0=lam_in[0:1, 0:2, :], in1=lam_in[0:1, 2:4, :], op=ALU.mult
             )
-            dots = const.tile([P, 2], F32)
-            nc.vector.reduce_sum(out=dots[0:1], in_=products[0:1], axis=AX.X)
-            exp_dots = const.tile([P, 2], F32)
+
+        def sum_lambdas():
+            nc.vector.reduce_sum(out=dots[0:1], in_=lam_products[0:1], axis=AX.X)
+
+        def exp_lambdas():
             nc.scalar.activation(out=exp_dots[0:1], in_=dots[0:1], func=ACT.Exp)
+
+        def subtract_lambdas():
             nc.vector.tensor_scalar(
                 out=lam_column[0:1, 0:1],
                 in0=exp_dots[0:1, 1:2],
@@ -188,7 +197,13 @@ def tile_mixerdiffattention_pb_t_kernel(
         def spread_neg_lam():
             bank = psum.tile([P, T], F32, tag="bank")
             nc.tensor.matmul(bank[:, 0:2], lhsT=first_row[:], rhs=lam_column[:], start=True, stop=True)
-            nc.vector.tensor_copy(out=neg_lam[:], in_=bank[:, 0:1])
+            neg_lam_bank.append(bank)
+
+        def take_neg_lam():
+            nc.vector.tensor_copy(out=neg_lam[:], in_=neg_lam_bank[0][:, 0:1])
+
+        neg_lam_bank = []
+        LAMBDA_STEPS = {0: multiply_lambdas, 1: sum_lambdas, 2: exp_lambdas, 3: subtract_lambdas, 4: spread_neg_lam}
 
         qT, kT, v_grouped = {}, {}, {}
         s_columns, neg_max, row_sum, weight = {}, {}, {}, {}
@@ -216,9 +231,9 @@ def tile_mixerdiffattention_pb_t_kernel(
                 )
                 qT[b, quarter // 2] = rows
 
-        def regroup_values(n, slot):
+        def regroup_values(n):
             b, quarter = divmod(n, 4)
-            keys_together = regrouped.tile([P, P, PACK], BF16, align_bytes=64, tag="regrouped%d" % slot)
+            keys_together = regrouped.tile([P, P, PACK], BF16, align_bytes=64, tag="regrouped%d" % (n if n < 4 else 0))
             nc.gpsimd.tensor_scalar(
                 out=keys_together[:],
                 in0=v_in[b][:, :, quarter * P : (quarter + 1) * P].rearrange("p t f -> p f t"),
@@ -239,17 +254,23 @@ def tile_mixerdiffattention_pb_t_kernel(
             )
 
         def move_values(b):
-            rows = P // PACK
-            for to, source in (
-                (part_codes[0][b % PART_BUFFERS], v_codes[b % VALUE_BUFFERS]),
-                (part_scales[b % PART_BUFFERS], v_scales[b % VALUE_BUFFERS]),
-            ):
-                nc.sync.dma_start(out=to[WORDS - rows :, :].bitcast(I32), in_=source[:rows, :].bitcast(I32))
+            for i, rows in ((1, 64), (0, 32)):
+                name, n = part_of(b, i)
+                first = 0 if name == "1 first" else WORDS - rows
+                to = slice(first, first + rows)
+                nc.sync.dma_start(
+                    out=part_codes[name][n][to, :].bitcast(I32), in_=v_codes[b % VALUE_BUFFERS][:rows, :].bitcast(I32)
+                )
+                if first > 0:
+                    nc.sync.dma_start(
+                        out=part_scales[name][n][to, :].bitcast(I32),
+                        in_=v_scales[b % VALUE_BUFFERS][:rows, :].bitcast(I32),
+                    )
 
         def copy_values(b):
             rows = 3 * P // PACK
             nc.gpsimd.tensor_copy(
-                out=part_codes[2][b % PART_BUFFERS][:rows, :], in_=v_codes[b % VALUE_BUFFERS][:rows, :]
+                out=part_codes["2"][b % PART_BUFFERS][:rows, :], in_=v_codes[b % VALUE_BUFFERS][:rows, :]
             )
 
         def half(h):
@@ -286,14 +307,13 @@ def tile_mixerdiffattention_pb_t_kernel(
                 row_sums = sums.tile([P, Q_TILES, GROUPS], F32, tag="row_sum")
                 row_sum[b] = row_sums
             stack = STACK_OF_TILE[i]
-            if i == 1:
-                e_stack[b, stack] = e_of_1[b % len(e_of_1)]
-            elif (b, stack) not in e_stack:
+            key = (b - b % 2 if i == 1 else b, stack)
+            if key not in e_stack:
                 e_tile = stacks.tile([P, GROUPS, PLANES, T // PLANES], BF16, tag="e_" + stack)
-                e_stack[b, stack] = e_tile
+                e_stack[key] = e_tile
             width = n_keys // PLANES
-            first = T // PLANES - width if i == 0 else 0
-            e_out = e_stack[b, stack][:, place, :, first : first + width]
+            first = T // PLANES - width if i == 0 or (i == 1 and b % 2 == 1) else 0
+            e_out = e_stack[key][:, place, :, first : first + width]
             nc.scalar.activation(
                 out=e_out.rearrange("p a (w c) -> p a w c", c=2),
                 in_=s_columns[h].rearrange("p (w a c) -> p a w c", a=PLANES, c=2),
@@ -344,20 +364,25 @@ def tile_mixerdiffattention_pb_t_kernel(
             )
             e_codes[b, stack], e_scales[b, stack] = codes, scales
 
+        def product_unit(n):
+            pair, m = divmod(n, PAIR)
+            return 2 * pair + PRODUCTS[m][0], PRODUCTS[m][1]
+
         def product(n, place):
-            b, i = n // Q_TILES, PRODUCT_ORDER[n % Q_TILES]
-            stack = STACK_OF_TILE[i]
+            b, i = product_unit(n)
+            key = (b - b % 2 if i == 1 else b, STACK_OF_TILE[i])
             queries = slice(place * P, (place + 1) * P)
             codes, scales = v_codes[b % VALUE_BUFFERS], v_scales[b % VALUE_BUFFERS]
-            if i in part_codes:
-                codes = part_codes[i][b % PART_BUFFERS]
-            if i == 0:
-                scales = part_scales[b % PART_BUFFERS]
+            if i != 3:
+                name, buffer = part_of(b, i)
+                codes = part_codes[name][buffer]
+                if name in part_scales:
+                    scales = part_scales[name][buffer]
             bank = psum.tile([P, F], F32, tag="bank")
             nc.tensor.matmul_mx(
                 out=bank[:],
-                lhsT=e_codes[b, stack][:, queries].bitcast(FP8X4),
-                lhsT_scale=e_scales[b, stack][:, queries],
+                lhsT=e_codes[key][:, queries].bitcast(FP8X4),
+                lhsT_scale=e_scales[key][:, queries],
                 rhs=codes[:].bitcast(FP8X4),
                 rhs_scale=scales[:],
                 start=True,
@@ -366,7 +391,7 @@ def tile_mixerdiffattention_pb_t_kernel(
             y_bank[b, i, place] = bank
 
         def take_product(n, place):
-            b, i = n // Q_TILES, PRODUCT_ORDER[n % Q_TILES]
+            b, i = product_unit(n)
             if place == 0:
                 result = results.tile([P, F], F32, tag="result")
                 nc.scalar.activation(
@@ -388,7 +413,7 @@ def tile_mixerdiffattention_pb_t_kernel(
         def input_quarters(t):
             if t < 0:
                 return {-2: (0, 1), -1: (2, 3)}[t]
-            return (t + Q_TILES,) if t + Q_TILES < 4 * B else ()
+            return (t + Q_TILES - 1, t + Q_TILES) if t % 2 == 1 and t + Q_TILES < 4 * B else ()
 
         def value_quarters(t):
             if t < 1:
@@ -396,6 +421,19 @@ def tile_mixerdiffattention_pb_t_kernel(
             if t < 3:
                 return [2 * t - 2, 2 * t - 1]
             return [t + 1] if t + 1 < 4 * B else []
+
+        def regroup_quarters(t):
+            if t == -1:
+                return [0, 1, 2, 3]
+            return [t + 1] if t >= 3 and t + 1 < 4 * B else []
+
+        def stacks_of_turn(t):
+            stacks_now = []
+            for turn, second, stack in TRANSPOSES:
+                pair, rest = divmod(t - turn, PAIR)
+                if rest == 0 and 0 <= pair < B // 2:
+                    stacks_now.append((2 * pair + second, stack))
+            return stacks_now
 
         def loads_of_turn(t):
             entry, turn = divmod(t + LOAD_LEAD, Q_TILES)
@@ -407,10 +445,6 @@ def tile_mixerdiffattention_pb_t_kernel(
         def step(t):
             n_2, n_1 = t - PRODUCT_LAG, t - PRODUCT_LAG - 1
             quarters = value_quarters(t)
-            b_e, e_turn = divmod(t - E_LAG, Q_TILES)
-            b_q, q_turn = divmod(t - QUANTISE_LAG, Q_TILES)
-            live_e = 0 <= b_e < B and e_turn < len(STACKS)
-            live_q = 0 <= b_q < B and q_turn < len(STACKS)
 
             if 0 <= n_2 < TURNS:
                 product(n_2, 0)
@@ -420,15 +454,15 @@ def tile_mixerdiffattention_pb_t_kernel(
                 scores(2 * t + 1)
             for n in input_quarters(t):
                 turn_input(n // 4, n % 4)
-            if live_e:
-                turn_e(b_e, STACKS[e_turn])
+            for key in stacks_of_turn(t):
+                turn_e(*key)
             if 0 <= t + 1 < TURNS:
                 scores(2 * t + 2)
 
             if t % Q_TILES == WEIGHT_LAG % Q_TILES and 0 <= t - WEIGHT_LAG < TURNS:
                 weight_group_2((t - WEIGHT_LAG) // Q_TILES)
-            for slot, n in enumerate(quarters):
-                regroup_values(n, slot)
+            for n in regroup_quarters(t):
+                regroup_values(n)
             if t % Q_TILES == MOVE_LAG % Q_TILES and 0 <= t - MOVE_LAG < TURNS:
                 copy_values((t - MOVE_LAG) // Q_TILES)
 
@@ -445,8 +479,8 @@ def tile_mixerdiffattention_pb_t_kernel(
                     take_input(n // 4, n % 4)
             if 0 <= t + 1 < TURNS:
                 row_maximum(2 * t + 2)
-            if live_q:
-                quantise_e(b_q, STACKS[q_turn])
+            for key in stacks_of_turn(t - QUANTISE_LAG):
+                quantise_e(*key)
             if t % Q_TILES == SUMS_LAG % Q_TILES and 0 <= t - SUMS_LAG < TURNS:
                 invert_row_sums((t - SUMS_LAG) // Q_TILES)
             for n in quarters:
@@ -461,13 +495,13 @@ def tile_mixerdiffattention_pb_t_kernel(
                     take_input(n // 4, n % 4)
             if 0 <= t < TURNS:
                 numerators(2 * t + 1)
-            if live_e:
-                take_e(b_e, STACKS[e_turn])
+            for key in stacks_of_turn(t):
+                take_e(*key)
 
         nc.vector.tensor_copy(out=mask_bf16[:], in_=mask_f32[:])
         for t in range(-2, TURNS + PRODUCT_LAG + 1):
-            if t == 1:
-                compute_neg_lam()
-            if t == 2:
-                spread_neg_lam()
             step(t)
+            if t in LAMBDA_STEPS:
+                LAMBDA_STEPS[t]()
+            if t == 4:
+                take_neg_lam()

@@ -45,7 +45,8 @@ SUMS_LAG = 4
 WEIGHT_LAG = 5
 VALUE_BUFFERS = 4
 MOVE_LAG = 3
-PART_BUFFERS = 2
+MOVES = ((3, 0, 0), (5, 0, 1), (7, 1, 1), (7, 1, 0))
+PART_BUFFERS = {"2": 2, "0": 2, "1 first": 1, "1 second": 1}
 LOADS_AT_ONCE = 6
 LOAD_LEAD = 6
 
@@ -100,22 +101,21 @@ def tile_mixerdiffattention_pb_t_kernel(
         v_codes = value_tiles("v_codes", U32, VALUE_BUFFERS)
         v_scales = value_tiles("v_scales", U8, VALUE_BUFFERS)
         part_codes, part_scales = {}, {}
-        for name in ("2", "0", "1 first", "1 second"):
-            part_codes[name] = value_tiles("part_codes_" + name.replace(" ", "_"), U32, PART_BUFFERS)
+        for name, count in PART_BUFFERS.items():
+            part_codes[name] = value_tiles("part_codes_" + name.replace(" ", "_"), U32, count)
         for name in ("0", "1 second"):
-            part_scales[name] = value_tiles("part_scales_" + name.replace(" ", "_"), U8, PART_BUFFERS)
+            part_scales[name] = value_tiles("part_scales_" + name.replace(" ", "_"), U8, PART_BUFFERS[name])
         for tile_list in [v_scales] + list(part_scales.values()):
             for v_tile in tile_list:
                 nc.vector.memset(v_tile[:].bitcast(I32), 0)
-        for name, tile_list in part_codes.items():
-            engine = nc.vector if name in part_scales else nc.gpsimd
-            for v_tile in tile_list:
-                engine.memset(v_tile[:].bitcast(F32), 0.0)
+        for name in ("2", "0"):
+            for v_tile in part_codes[name]:
+                nc.gpsimd.memset(v_tile[:].bitcast(F32), 0.0)
 
         def part_of(b, i):
             if i == 1:
-                return ("1 first", "1 second")[b % 2], b // 2 % PART_BUFFERS
-            return str(i), b % PART_BUFFERS
+                return ("1 first", "1 second")[b % 2], 0
+            return str(i), b % 2
 
         q_heads, k_heads, v_in = [], [], []
         lam_in = const.tile([P, 4, LAM_LEN], BF16)
@@ -253,24 +253,23 @@ def tile_mixerdiffattention_pb_t_kernel(
                 in_=v_grouped[n][:].rearrange("p f t -> p (f t)"),
             )
 
-        def move_values(b):
-            for i, rows in ((1, 64), (0, 32)):
-                name, n = part_of(b, i)
-                first = 0 if name == "1 first" else WORDS - rows
-                to = slice(first, first + rows)
+        def move_values(b, i):
+            rows = {1: 64, 0: 32}[i]
+            name, n = part_of(b, i)
+            first = 0 if name == "1 first" else WORDS - rows
+            to = slice(first, first + rows)
+            nc.sync.dma_start(
+                out=part_codes[name][n][to, :].bitcast(I32), in_=v_codes[b % VALUE_BUFFERS][:rows, :].bitcast(I32)
+            )
+            if first > 0:
                 nc.sync.dma_start(
-                    out=part_codes[name][n][to, :].bitcast(I32), in_=v_codes[b % VALUE_BUFFERS][:rows, :].bitcast(I32)
+                    out=part_scales[name][n][to, :].bitcast(I32), in_=v_scales[b % VALUE_BUFFERS][:rows, :].bitcast(I32)
                 )
-                if first > 0:
-                    nc.sync.dma_start(
-                        out=part_scales[name][n][to, :].bitcast(I32),
-                        in_=v_scales[b % VALUE_BUFFERS][:rows, :].bitcast(I32),
-                    )
 
         def copy_values(b):
             rows = 3 * P // PACK
             nc.gpsimd.tensor_copy(
-                out=part_codes["2"][b % PART_BUFFERS][:rows, :], in_=v_codes[b % VALUE_BUFFERS][:rows, :]
+                out=part_codes["2"][b % 2][:rows, :], in_=v_codes[b % VALUE_BUFFERS][:rows, :]
             )
 
         def half(h):
@@ -348,7 +347,8 @@ def tile_mixerdiffattention_pb_t_kernel(
 
         def take_e(b, stack):
             keys_together = grouped.tile([P, GROUPS * P, PACK], BF16, align_bytes=64, tag="grouped")
-            nc.scalar.copy(
+            copy = nc.vector.tensor_copy if (b, stack) == (B - 2, "1") else nc.scalar.copy
+            copy(
                 out=keys_together[:].bitcast(F32).rearrange("p (n r) a -> p n r a", n=GROUPS),
                 in_=e_bank[b, stack][:].rearrange("p (n a r) -> p n r a", n=GROUPS, a=PLANES),
             )
@@ -470,8 +470,10 @@ def tile_mixerdiffattention_pb_t_kernel(
                 row_maximum(2 * t + 1)
             if 0 <= n_1 < TURNS:
                 take_product(n_1, 1)
-            if t % Q_TILES == MOVE_LAG % Q_TILES and 0 <= t - MOVE_LAG < TURNS:
-                move_values((t - MOVE_LAG) // Q_TILES)
+            for turn, second, i in MOVES:
+                pair, rest = divmod(t - turn, PAIR)
+                if rest == 0 and 0 <= pair < B // 2:
+                    move_values(2 * pair + second, i)
             for n in loads_of_turn(t):
                 load(n)
             for n in input_quarters(t):
@@ -479,12 +481,18 @@ def tile_mixerdiffattention_pb_t_kernel(
                     take_input(n // 4, n % 4)
             if 0 <= t + 1 < TURNS:
                 row_maximum(2 * t + 2)
+            for b, stack in stacks_of_turn(t):
+                if (b, stack) == (B - 2, "1"):
+                    take_e(b, stack)
             for key in stacks_of_turn(t - QUANTISE_LAG):
                 quantise_e(*key)
             if t % Q_TILES == SUMS_LAG % Q_TILES and 0 <= t - SUMS_LAG < TURNS:
                 invert_row_sums((t - SUMS_LAG) // Q_TILES)
             for n in quarters:
                 quantise_values(n)
+
+            if t in (-2, -1):
+                nc.vector.memset(part_codes["1 first" if t == -2 else "1 second"][0][:].bitcast(I32), 0)
 
             if 0 <= t < TURNS:
                 numerators(2 * t)
@@ -495,8 +503,9 @@ def tile_mixerdiffattention_pb_t_kernel(
                     take_input(n // 4, n % 4)
             if 0 <= t < TURNS:
                 numerators(2 * t + 1)
-            for key in stacks_of_turn(t):
-                take_e(*key)
+            for b, stack in stacks_of_turn(t):
+                if not ((b, stack) == (B - 2, "1")):
+                    take_e(b, stack)
 
         nc.vector.tensor_copy(out=mask_bf16[:], in_=mask_f32[:])
         for t in range(-2, TURNS + PRODUCT_LAG + 1):

import math
from contextlib import ExitStack

import concourse.mybir as mybir
from concourse.masks import make_identity

F32 = mybir.dt.float32
BF16 = mybir.dt.bfloat16
U32 = mybir.dt.uint32
I32 = mybir.dt.int32
U8 = mybir.dt.uint8
FP8X4 = mybir.dt.float8_e4m3fn_x4
ALU = mybir.AluOpType
ACT = mybir.ActivationFunctionType
AX = mybir.AxisListType

P = 128
PACK = 4
B = 8
T = 512
GROUPS = 2
HD = 256
F = 512
LAM_LEN = 128
Q_TILES = T // P
PLANES = 2
WORDS = T // PACK
SCORE_SCALE = 1.0 / math.sqrt(HD)
LAMBDA_INIT = 0.8 - 0.6 * math.exp(-0.3 * 0)
MASKED = -1.0e30
HEAD_AT_PLACE = (1, 0)

FLOPS = B * GROUPS * (2 * T * T * HD + 2 * T * T * F)

TILE_ORDER = (0, 3, 1, 2)
STACK_OF_TILE = {3: "3", 2: "20", 0: "20", 1: "1"}
HALVES = B * Q_TILES * GROUPS
TURNS = HALVES // 2
PAIR = 2 * Q_TILES
TRANSPOSES = ((3, 0, "3"), (5, 0, "20"), (7, 1, "3"), (8, 0, "1"), (9, 1, "20"))
QUANTISE_LAG = 1
PRODUCTS = ((0, 3), (0, 2), (0, 0), (1, 3), (0, 1), (1, 1), (1, 2), (1, 0))
PRODUCT_LAG = 7
SUMS_LAG = 4
WEIGHT_LAG = 5
VALUE_BUFFERS = 4
MOVE_LAG = 3
MOVES = ((3, 0, 0), (5, 0, 1), (7, 1, 1), (7, 1, 0))
PART_BUFFERS = {"2": 2, "0": 2, "1 first": 1, "1 second": 1}
LOADS_AT_ONCE = 6
LOAD_LEAD = 6


def tile_mixerdiffattention_pb_t_kernel(
    tc, q_rot, k_rot, v, lambda_q1, lambda_k1, lambda_q2, lambda_k2, out
):
    nc = tc.nc
    with ExitStack() as ctx:
        ctx.enter_context(tc.manual_schedule())

        const = ctx.enter_context(tc.tile_pool(name="const", bufs=1))
        loads = ctx.enter_context(tc.tile_pool(name="loads", bufs=B))
        turned_inputs = ctx.enter_context(tc.tile_pool(name="turned_inputs", bufs=2 * GROUPS))
        regrouped = ctx.enter_context(tc.tile_pool(name="regrouped", bufs=1))
        stacks = ctx.enter_context(tc.tile_pool(name="stacks", bufs=2))
        grouped = ctx.enter_context(tc.tile_pool(name="grouped", bufs=3))
        quantised = ctx.enter_context(tc.tile_pool(name="quantised", bufs=5))
        stats = ctx.enter_context(tc.tile_pool(name="stats", bufs=8))
        sums = ctx.enter_context(tc.tile_pool(name="sums", bufs=4))
        results = ctx.enter_context(tc.tile_pool(name="results", bufs=8))
        psum = ctx.enter_context(tc.psum_pool(name="psum", bufs=8))

        ident_f32 = const.tile([P, P], F32)
        make_identity(nc, ident_f32[:])
        ident_bf16 = const.tile([P, P], BF16)
        make_identity(nc, ident_bf16[:])
        mask_f32 = const.tile([P, P], F32)
        nc.gpsimd.memset(mask_f32[:], 0.0)
        nc.gpsimd.affine_select(
            out=mask_f32[:],
            in_=mask_f32[:],
            compare_op=ALU.is_ge,
            fill=MASKED,
            base=0,
            pattern=[[-1, P]],
            channel_multiplier=1,
        )
        mask_bf16 = const.tile([P, P], BF16)
        zero_column = const.tile([P, 1], F32)
        nc.vector.memset(zero_column[:], 0.0)
        one_column = const.tile([P, 1], F32)
        nc.scalar.activation(out=one_column[:], in_=zero_column[:], func=ACT.Exp)

        def value_tiles(name, dtype, count):
            tiles = []
            for n in range(count):
                v_tile = const.tile([P, F], dtype, name="%s_%d" % (name, n), align_bytes=256)
                tiles.append(v_tile)
            return tiles

        v_codes = value_tiles("v_codes", U32, VALUE_BUFFERS)
        v_scales = value_tiles("v_scales", U8, VALUE_BUFFERS)
        part_codes, part_scales = {}, {}
        for name, count in PART_BUFFERS.items():
            part_codes[name] = value_tiles("part_codes_" + name.replace(" ", "_"), U32, count)
        for name in ("0", "1 second"):
            part_scales[name] = value_tiles("part_scales_" + name.replace(" ", "_"), U8, PART_BUFFERS[name])
        for tile_list in [v_scales] + list(part_scales.values()):
            for v_tile in tile_list:
                nc.vector.memset(v_tile[:].bitcast(I32), 0)
        for name in ("2", "0"):
            for v_tile in part_codes[name]:
                nc.gpsimd.memset(v_tile[:].bitcast(F32), 0.0)

        def part_of(b, i):
            if i == 1:
                return ("1 first", "1 second")[b % 2], 0
            return str(i), b % 2

        q_heads, k_heads, v_in = [], [], []
        lam_in = const.tile([P, 4, LAM_LEN], BF16)

        def load_first_entry():
            first = {}
            for head in HEAD_AT_PLACE:
                for letter, source in (("k", k_rot), ("q", q_rot)):
                    part = const.tile([P, Q_TILES, HD], BF16, name="first_%s%d" % (letter, head))
                    nc.sync.dma_start(
                        out=part[:], in_=source[0, :, head, :].rearrange("(j p) d -> p j d", p=P)
                    )
                    first[letter, head] = part[:]
            q_heads.append([first["q", head] for head in range(GROUPS)])
            k_heads.append([first["k", head] for head in range(GROUPS)])

        def load_both_heads(letter, source, b, heads):
            both = loads.tile([P, Q_TILES, GROUPS * HD], BF16, tag=letter)
            nc.sync.dma_start(out=both[:], in_=source[b].rearrange("(j p) h d -> p j (h d)", p=P))
            heads.append([both[:, :, head * HD : (head + 1) * HD] for head in range(GROUPS)])

        def load_values(b):
            v_sb = loads.tile([P, PACK, F], BF16, tag="v")
            nc.sync.dma_start(out=v_sb[:], in_=v[b].rearrange("(p t) o f -> p t (o f)", t=PACK))
            v_in.append(v_sb)

        load_first_entry()
        for n, vec in enumerate((lambda_q1, lambda_q2, lambda_k1, lambda_k2)):
            nc.sync.dma_start(out=lam_in[0:1, n, :], in_=vec.rearrange("(o n) -> o n", o=1))
        later_loads = []
        for b in range(1, B):
            later_loads += [("k", b), ("v", b - 1), ("q", b)]
        later_loads.append(("v", B - 1))

        def load(n):
            letter, b = later_loads[n]
            if letter == "v":
                load_values(b)
            elif letter == "k":
                load_both_heads("k", k_rot, b, k_heads)
            else:
                load_both_heads("q", q_rot, b, q_heads)

        for n in range(LOADS_AT_ONCE):
            load(n)

        neg_lam = const.tile([P, 1], F32)
        lam_column = const.tile([P, 2], F32)
        nc.vector.memset(lam_column[:], 0.0)
        first_row = const.tile([P, P], F32)
        nc.vector.memset(first_row[:], 0.0)
        nc.vector.memset(first_row[0:1, :], 1.0)

        lam_products = const.tile([P, 2, LAM_LEN], F32)
        dots = const.tile([P, 2], F32)
        exp_dots = const.tile([P, 2], F32)

        def multiply_lambdas():
            nc.vector.tensor_tensor(
                out=lam_products[0:1], in0=lam_in[0:1, 0:2, :], in1=lam_in[0:1, 2:4, :], op=ALU.mult
            )

        def sum_lambdas():
            nc.vector.reduce_sum(out=dots[0:1], in_=lam_products[0:1], axis=AX.X)

        def exp_lambdas():
            nc.scalar.activation(out=exp_dots[0:1], in_=dots[0:1], func=ACT.Exp)

        def subtract_lambdas():
            nc.vector.tensor_scalar(
                out=lam_column[0:1, 0:1],
                in0=exp_dots[0:1, 1:2],
                scalar1=exp_dots[0:1, 0:1],
                scalar2=-LAMBDA_INIT,
                op0=ALU.subtract,
                op1=ALU.add,
            )

        def spread_neg_lam():
            bank = psum.tile([P, T], F32, tag="bank")
            nc.tensor.matmul(bank[:, 0:2], lhsT=first_row[:], rhs=lam_column[:], start=True, stop=True)
            neg_lam_bank.append(bank)

        def take_neg_lam():
            nc.vector.tensor_copy(out=neg_lam[:], in_=neg_lam_bank[0][:, 0:1])

        neg_lam_bank = []
        LAMBDA_STEPS = {0: multiply_lambdas, 1: sum_lambdas, 2: exp_lambdas, 3: subtract_lambdas, 4: spread_neg_lam}

        qT, kT, v_grouped = {}, {}, {}
        s_columns, neg_max, row_sum, weight = {}, {}, {}, {}
        e_stack, e_bank, e_grouped, e_codes, e_scales = {}, {}, {}, {}, {}
        kq_bank, y_bank, result_of = {}, {}, {}

        def turn_input(b, quarter):
            place = quarter // 2
            source = (k_heads, q_heads)[quarter % 2]
            words = source[b][HEAD_AT_PLACE[place]].bitcast(F32)
            bank = psum.tile([P, T], F32, tag="bank")
            for j in range(Q_TILES):
                nc.tensor.transpose(bank[:, j * P : (j + 1) * P], words[:, j, :], ident_f32[:])
            kq_bank[b, quarter] = bank

        def take_input(b, quarter):
            bank = kq_bank[b, quarter]
            rows = turned_inputs.tile([P, T, 2], BF16, tag="turned%d" % (quarter % 2))
            if quarter % 2 == 0:
                nc.scalar.copy(out=rows[:].bitcast(F32).rearrange("p r w -> p (r w)"), in_=bank[:])
                kT[b, quarter // 2] = rows
            else:
                nc.vector.tensor_scalar_mul(
                    out=rows[:].rearrange("p r w -> p (r w)"), in0=bank[:].bitcast(BF16), scalar1=SCORE_SCALE
                )
                qT[b, quarter // 2] = rows

        def regroup_values(n):
            b, quarter = divmod(n, 4)
            keys_together = regrouped.tile([P, P, PACK], BF16, align_bytes=64, tag="regrouped%d" % (n if n < 4 else 0))
            nc.gpsimd.tensor_scalar(
                out=keys_together[:],
                in0=v_in[b][:, :, quarter * P : (quarter + 1) * P].rearrange("p t f -> p f t"),
                scalar1=1.0,
                scalar2=0.0,
                op0=ALU.mult,
                op1=ALU.add,
            )
            v_grouped[n] = keys_together

        def quantise_values(n):
            b, quarter = divmod(n, 4)
            features = slice(quarter * P, (quarter + 1) * P)
            nc.vector.quantize_mx(
                out=v_codes[b % VALUE_BUFFERS][:, features].bitcast(FP8X4),
                scales=v_scales[b % VALUE_BUFFERS][:, features],
                in_=v_grouped[n][:].rearrange("p f t -> p (f t)"),
            )

        def move_values(b, i):
            rows = {1: 64, 0: 32}[i]
            name, n = part_of(b, i)
            first = 0 if name == "1 first" else WORDS - rows
            to = slice(first, first + rows)
            nc.sync.dma_start(
                out=part_codes[name][n][to, :].bitcast(I32), in_=v_codes[b % VALUE_BUFFERS][:rows, :].bitcast(I32)
            )
            if first > 0:
                nc.sync.dma_start(
                    out=part_scales[name][n][to, :].bitcast(I32), in_=v_scales[b % VALUE_BUFFERS][:rows, :].bitcast(I32)
                )

        def copy_values(b):
            rows = 3 * P // PACK
            nc.gpsimd.tensor_copy(
                out=part_codes["2"][b % 2][:rows, :], in_=v_codes[b % VALUE_BUFFERS][:rows, :]
            )

        def half(h):
            turn, second = divmod(h, 2)
            two_tiles, place = divmod(turn, GROUPS)
            b, n = divmod(2 * two_tiles + second, Q_TILES)
            return b, TILE_ORDER[n], place

        def scores(h):
            b, i, place = half(h)
            rows = slice(i * P, (i + 1) * P)
            n_keys = (i + 1) * P
            queries, keys = qT[b, place], kT[b, place]
            bank = psum.tile([P, T], F32, tag="bank")
            s = bank[:, :n_keys]
            nc.tensor.matmul(s, lhsT=queries[:, rows, 0], rhs=keys[:, :n_keys, 0], start=True, stop=False)
            nc.tensor.matmul(bank[:, rows], lhsT=ident_bf16[:], rhs=mask_bf16[:], start=False, stop=False)
            nc.tensor.matmul(s, lhsT=queries[:, rows, 1], rhs=keys[:, :n_keys, 1], start=False, stop=True)
            s_columns[h] = s

        def row_maximum(h):
            b, i, place = half(h)
            if place == 0:
                maxima = stats.tile([P, GROUPS], F32, tag="neg_max")
                neg_max[b, i] = maxima
            nc.vector.reduce_max(
                out=neg_max[b, i][:, place : place + 1], in_=s_columns[h], axis=AX.X, negate=True
            )

        def numerators(h):
            b, i, place = half(h)
            n_keys = (i + 1) * P
            if b not in row_sum:
                row_sums = sums.tile([P, Q_TILES, GROUPS], F32, tag="row_sum")
                row_sum[b] = row_sums
            stack = STACK_OF_TILE[i]
            key = (b - b % 2 if i == 1 else b, stack)
            if key not in e_stack:
                e_tile = stacks.tile([P, GROUPS, PLANES, T // PLANES], BF16, tag="e_" + stack)
                e_stack[key] = e_tile
            width = n_keys // PLANES
            first = T // PLANES - width if i == 0 or (i == 1 and b % 2 == 1) else 0
            e_out = e_stack[key][:, place, :, first : first + width]
            nc.scalar.activation(
                out=e_out.rearrange("p a (w c) -> p a w c", c=2),
                in_=s_columns[h].rearrange("p (w a c) -> p a w c", a=PLANES, c=2),
                func=ACT.Exp,
                bias=neg_max[b, i][:, place : place + 1],
                accum_out=row_sum[b][:, i, place : place + 1],
            )

        def invert_row_sums(b):
            factors = sums.tile([P, Q_TILES, GROUPS], F32, tag="weight")
            nc.vector.reciprocal(out=factors[:], in_=row_sum[b][:])
            weight[b] = factors

        def weight_group_2(b):
            nc.gpsimd.tensor_scalar(
                out=weight[b][:, :, 0],
                in0=weight[b][:, :, 0],
                scalar1=neg_lam[:, 0:1],
                scalar2=0.0,
                op0=ALU.mult,
                op1=ALU.add,
            )

        def turn_e(b, stack):
            e_words = e_stack[b, stack][:].bitcast(F32)
            bank = psum.tile([P, T], F32, tag="bank")
            for place in range(GROUPS):
                for plane in range(PLANES):
                    column = (PLANES * place + plane) * P
                    nc.tensor.transpose(bank[:, column : column + P], e_words[:, place, plane, :], ident_f32[:])
            e_bank[b, stack] = bank

        def take_e(b, stack):
            keys_together = grouped.tile([P, GROUPS * P, PACK], BF16, align_bytes=64, tag="grouped")
            copy = nc.vector.tensor_copy if (b, stack) == (B - 2, "1") else nc.scalar.copy
            copy(
                out=keys_together[:].bitcast(F32).rearrange("p (n r) a -> p n r a", n=GROUPS),
                in_=e_bank[b, stack][:].rearrange("p (n a r) -> p n r a", n=GROUPS, a=PLANES),
            )
            e_grouped[b, stack] = keys_together

        def quantise_e(b, stack):
            codes = quantised.tile([P, GROUPS * P], U32, align_bytes=64, tag="codes")
            scales = quantised.tile([P, GROUPS * P], U8, align_bytes=64, tag="scales")
            nc.vector.quantize_mx(
                out=codes[:].bitcast(FP8X4),
                scales=scales[:],
                in_=e_grouped[b, stack][:].rearrange("p r t -> p (r t)"),
            )
            e_codes[b, stack], e_scales[b, stack] = codes, scales

        def product_unit(n):
            pair, m = divmod(n, PAIR)
            return 2 * pair + PRODUCTS[m][0], PRODUCTS[m][1]

        def product(n, place):
            b, i = product_unit(n)
            key = (b - b % 2 if i == 1 else b, STACK_OF_TILE[i])
            queries = slice(place * P, (place + 1) * P)
            codes, scales = v_codes[b % VALUE_BUFFERS], v_scales[b % VALUE_BUFFERS]
            if i != 3:
                name, buffer = part_of(b, i)
                codes = part_codes[name][buffer]
                if name in part_scales:
                    scales = part_scales[name][buffer]
            bank = psum.tile([P, F], F32, tag="bank")
            nc.tensor.matmul_mx(
                out=bank[:],
                lhsT=e_codes[key][:, queries].bitcast(FP8X4),
                lhsT_scale=e_scales[key][:, queries],
                rhs=codes[:].bitcast(FP8X4),
                rhs_scale=scales[:],
                start=True,
                stop=True,
            )
            y_bank[b, i, place] = bank

        def take_product(n, place):
            b, i = product_unit(n)
            if place == 0:
                result = results.tile([P, F], F32, tag="result")
                nc.scalar.activation(
                    out=result[:], in_=y_bank[b, i, 0][:], func=ACT.Copy, scale=weight[b][:, i, 0:1]
                )
                result_of[b, i] = result
            else:
                nc.vector.scalar_tensor_tensor(
                    out=result_of[b, i][:],
                    in0=y_bank[b, i, 1][:],
                    scalar=weight[b][:, i, 1:2],
                    in1=result_of[b, i][:],
                    op0=ALU.mult,
                    op1=ALU.add,
                )
                nc.sync.dma_start(out=out[b, i * P : (i + 1) * P, :], in_=result_of[b, i][:])


        def input_quarters(t):
            if t < 0:
                return {-2: (0, 1), -1: (2, 3)}[t]
            return (t + Q_TILES - 1, t + Q_TILES) if t % 2 == 1 and t + Q_TILES < 4 * B else ()

        def value_quarters(t):
            if t < 1:
                return []
            if t < 3:
                return [2 * t - 2, 2 * t - 1]
            return [t + 1] if t + 1 < 4 * B else []

        def regroup_quarters(t):
            if t == -1:
                return [0, 1, 2, 3]
            return [t + 1] if t >= 3 and t + 1 < 4 * B else []

        def stacks_of_turn(t):
            stacks_now = []
            for turn, second, stack in TRANSPOSES:
                pair, rest = divmod(t - turn, PAIR)
                if rest == 0 and 0 <= pair < B // 2:
                    stacks_now.append((2 * pair + second, stack))
            return stacks_now

        def loads_of_turn(t):
            entry, turn = divmod(t + LOAD_LEAD, Q_TILES)
            n = 3 * entry + turn
            if turn < 3 and LOADS_AT_ONCE <= n < len(later_loads):
                return [n]
            return []

        def step(t):
            n_2, n_1 = t - PRODUCT_LAG, t - PRODUCT_LAG - 1
            quarters = value_quarters(t)

            if 0 <= n_2 < TURNS:
                product(n_2, 0)
            if 0 <= n_1 < TURNS:
                product(n_1, 1)
            if 0 <= t < TURNS:
                scores(2 * t + 1)
            for n in input_quarters(t):
                turn_input(n // 4, n % 4)
            for key in stacks_of_turn(t):
                turn_e(*key)
            if 0 <= t + 1 < TURNS:
                scores(2 * t + 2)

            if t % Q_TILES == WEIGHT_LAG % Q_TILES and 0 <= t - WEIGHT_LAG < TURNS:
                weight_group_2((t - WEIGHT_LAG) // Q_TILES)
            for n in regroup_quarters(t):
                regroup_values(n)
            if t % Q_TILES == MOVE_LAG % Q_TILES and 0 <= t - MOVE_LAG < TURNS:
                copy_values((t - MOVE_LAG) // Q_TILES)

            if 0 <= t < TURNS:
                row_maximum(2 * t + 1)
            if 0 <= n_1 < TURNS:
                take_product(n_1, 1)
            for turn, second, i in MOVES:
                pair, rest = divmod(t - turn, PAIR)
                if rest == 0 and 0 <= pair < B // 2:
                    move_values(2 * pair + second, i)
            for n in loads_of_turn(t):
                load(n)
            for n in input_quarters(t):
                if n % 2 == 1:
                    take_input(n // 4, n % 4)
            if 0 <= t + 1 < TURNS:
                row_maximum(2 * t + 2)
            for b, stack in stacks_of_turn(t):
                if (b, stack) == (B - 2, "1"):
                    take_e(b, stack)
            for key in stacks_of_turn(t - QUANTISE_LAG):
                quantise_e(*key)
            if t % Q_TILES == SUMS_LAG % Q_TILES and 0 <= t - SUMS_LAG < TURNS:
                invert_row_sums((t - SUMS_LAG) // Q_TILES)
            for n in quarters:
                quantise_values(n)

            if t in (-2, -1):
                nc.vector.memset(part_codes["1 first" if t == -2 else "1 second"][0][:].bitcast(I32), 0)

            if 0 <= t < TURNS:
                numerators(2 * t)
            if 0 <= n_2 < TURNS:
                take_product(n_2, 0)
            for n in input_quarters(t):
                if n % 2 == 0:
                    take_input(n // 4, n % 4)
            if 0 <= t < TURNS:
                numerators(2 * t + 1)
            for b, stack in stacks_of_turn(t):
                if not ((b, stack) == (B - 2, "1")):
                    take_e(b, stack)

        nc.vector.tensor_copy(out=mask_bf16[:], in_=mask_f32[:])
        for t in range(-2, TURNS + PRODUCT_LAG + 1):
            step(t)
            if t in LAMBDA_STEPS:
                LAMBDA_STEPS[t]()
            if t == 4:
                take_neg_lam()
